import numpy as np
import ml_dtypes


def mxq(x, axis, fmt="e4m3"):
    dtype, down = {"e4m3": (ml_dtypes.float8_e4m3fn, 7), "e5m2": (ml_dtypes.float8_e5m2, 14)}[fmt]
    v = np.moveaxis(np.asarray(x, np.float32).astype(ml_dtypes.bfloat16).astype(np.float64), axis, -1)
    blocks = v.reshape(v.shape[:-1] + (-1, 32))
    amax = np.abs(blocks).max(-1, keepdims=True)
    byte = np.maximum(np.where(amax > 0, np.frexp(amax)[1] - 1 + 127, 0) - down, 1)
    scale = np.exp2(byte - 127.0)
    codes = (blocks / scale).astype(np.float32).astype(dtype).astype(np.float64)
    return np.moveaxis((codes * scale).reshape(v.shape), -1, axis)


WIDE = False


def mx_kscale(k):
    if not WIDE:
        return np.ones(k)
    levels = np.array([10, -10, 5, -5, 0])
    a = np.random.permutation(np.resize(levels, k // 512 * 4)).reshape(k // 512, 4)
    idx = np.arange(k)
    return np.exp2(a[idx // 512, idx % 128 // 32])


BF16 = ml_dtypes.bfloat16


def bf(x):
    return np.asarray(x, np.float32).astype(BF16)


def f64(x):
    return np.asarray(x).astype(np.float64)


B, N, R, F = 144, 8, 512, 512
GAMMA = 10.0
STEP = 0.1
LOG2 = np.log(2.0)


def ssp(v):
    return np.maximum(v, 0.0) + np.log(1.0 + np.exp(-np.abs(v))) - LOG2


def setup_inputs():
    t = mx_kscale(F)
    t = t / t.min()
    return {"x": bf(np.random.standard_normal((B, N, F))),
            "distances": bf(np.random.uniform(0.0, STEP * R, (B, N, N))),
            "W1": bf(np.random.standard_normal((R, F)) * 0.5 * t[None, :]),
            "b1": bf(np.random.standard_normal(F) * 0.2 * t),
            "W2": bf(np.random.standard_normal((F, F)) * 2.0 / np.sqrt(F) / t[:, None]),
            "b2": bf(np.random.standard_normal(F) * 0.2)}


def reference(x, distances, W1, b1, W2, b2):
    centers = STEP * np.arange(R)
    e_k = np.exp(-GAMMA * (f64(distances)[..., None] - centers) ** 2)
    h = ssp((mxq(e_k, 3, "e4m3") @ mxq(f64(W1), 0, "e4m3")) + f64(b1))
    w_l = ssp((mxq(h, 3, "e4m3") @ mxq(f64(W2), 0, "e4m3")) + f64(b2))
    return np.sum(f64(x)[:, :, None, :] * w_l, axis=2)

@@ -1,0 +1,304 @@
+import math
+
+import concourse.mybir as mybir
+from concourse.masks import make_identity
+
+F32 = mybir.dt.float32
+BF16 = mybir.dt.bfloat16
+I32 = mybir.dt.int32
+U32 = mybir.dt.uint32
+U8 = mybir.dt.uint8
+FP8X4 = mybir.dt.float8_e4m3fn_x4
+ACT = mybir.ActivationFunctionType
+ALU = mybir.AluOpType
+
+P = 128
+PACK = 4
+ATOMS = 8
+ATOM_ROWS = 144 * ATOMS
+PAIRS = ATOM_ROWS * ATOMS
+FEATURES = P * PACK
+
+INV_STEP = 10.0
+WIDTH = 0.1
+LN2 = math.log(2.0)
+TINY = 2.0**-62
+
+BASIS_STEP = 1024
+BASIS_STEPS = PAIRS // BASIS_STEP
+CHUNK = 512
+CHUNKS = PAIRS // CHUNK
+BATCH = 3
+BATCHES = CHUNKS // BATCH
+OUT_TILES = ATOM_ROWS // P
+CHUNKS_PER_OUT_TILE = P * ATOMS // CHUNK
+
+HIDDEN = 0
+FILTER = 1
+
+FLOPS = 2 * 2 * PAIRS * FEATURES * FEATURES
+
+
+def tile_cfconv_pa_t_kernel(tc, x, distances, W1, b1, W2, b2, out):
+    nc = tc.nc
+    d_flat = distances.rearrange("b i j -> (b i j)")
+    x_rows = x.rearrange("b i f -> (b i) f")
+    out_rows = out.rearrange("b i f -> (b i) f")
+
+    with tc.manual_schedule(), tc.tile_pool(name="keep", bufs=1) as keep, tc.psum_pool(name="psum", bufs=4) as psum:
+        moving_codes = [
+            keep.tile([P, PAIRS], U32, name="basis_codes", align_bytes=64),
+            keep.tile([P, PAIRS], U32, name="hidden_codes", align_bytes=64),
+        ]
+        moving_scales = [
+            keep.tile([P, PAIRS], U8, name="basis_scales", align_bytes=64),
+            keep.tile([P, PAIRS], U8, name="hidden_scales", align_bytes=64),
+        ]
+        weight_codes = [
+            keep.tile([P, FEATURES], U32, name="w1_codes", align_bytes=64),
+            keep.tile([P, FEATURES], U32, name="w2_codes", align_bytes=64),
+        ]
+        weight_scales = [
+            keep.tile([P, FEATURES], U8, name="w1_scales", align_bytes=64),
+            keep.tile([P, FEATURES], U8, name="w2_scales", align_bytes=64),
+        ]
+
+        centre_int = keep.tile([P, PACK], I32, name="centre_int")
+        nc.gpsimd.iota(centre_int[:], pattern=[[1, PACK]], base=0, channel_multiplier=PACK)
+        centre = keep.tile([P, PACK], F32, name="centre")
+        nc.vector.tensor_copy(out=centre[:], in_=centre_int[:])
+        minus_centre = keep.tile([P, PACK], F32, name="minus_centre")
+        nc.vector.tensor_scalar(out=minus_centre[:], in0=centre[:], scalar1=-1.0, scalar2=None, op0=ALU.mult)
+        t_squared = keep.tile([P, PACK], F32, name="t_squared")
+        for t in range(PACK):
+            nc.vector.memset(t_squared[:, t : t + 1], float(t * t))
+        exp_bias = keep.tile([P, PACK], F32, name="exp_bias")
+        nc.vector.tensor_scalar(out=exp_bias[:], in0=t_squared[:], scalar1=-WIDTH, scalar2=None, op0=ALU.mult)
+        tiny = keep.tile([P, 1], F32, name="tiny")
+        nc.vector.memset(tiny[:], TINY)
+        identity = keep.tile([P, P], F32, name="identity")
+        make_identity(nc, identity[:])
+
+        minus_bias = [keep.tile([P, PACK], F32, name="minus_b1"), keep.tile([P, PACK], F32, name="minus_b2")]
+        guard_bias = [keep.tile([P, PACK], F32, name="guard_b1"), keep.tile([P, PACK], F32, name="guard_b2")]
+
+        with tc.tile_pool(name="basis", bufs=2) as work:
+            d_all = work.tile([P, PAIRS], BF16, name="d_all", bufs=1)
+
+            def load_distances(a):
+                cols = slice(a * BASIS_STEP, (a + 1) * BASIS_STEP)
+                nc.sync.dma_start(out=d_all[:, cols], in_=d_flat[cols].partition_broadcast(P))
+
+            load_distances(0)
+            load_distances(1)
+            raw_weights = []
+            raw_biases = []
+            for layer, (weight, bias) in enumerate(((W1, b1), (W2, b2))):
+                raw_w = work.tile([P, PACK, FEATURES], BF16, name="raw_w")
+                nc.sync.dma_start(out=raw_w[:], in_=weight.rearrange("(p j) f -> p j f", j=PACK))
+                raw_weights.append(raw_w)
+                raw_b = work.tile([P, PACK], BF16, name="raw_b")
+                nc.sync.dma_start(out=raw_b[:], in_=bias.rearrange("(c m) -> c m", m=PACK))
+                raw_biases.append(raw_b)
+            for a in range(2, BASIS_STEPS):
+                load_distances(a)
+
+            squares = {}
+            planes = {}
+            grouped = {}
+
+            def square_step(a):
+                cols = slice(a * BASIS_STEP, (a + 1) * BASIS_STEP)
+                sq = work.tile([P, PACK, BASIS_STEP], F32, name="sq")
+                for t in range(2):
+                    nc.scalar.activation(
+                        out=sq[:, t, :], in_=d_all[:, cols], func=ACT.Square,
+                        scale=INV_STEP, bias=minus_centre[:, t : t + 1],
+                    )
+                z0 = work.tile([P, BASIS_STEP], F32, name="z0")
+                nc.gpsimd.tensor_scalar(
+                    out=z0[:], in0=d_all[:, cols], scalar1=INV_STEP, scalar2=centre[:, 0:1],
+                    op0=ALU.mult, op1=ALU.subtract,
+                )
+                for t in range(2, PACK):
+                    nc.vector.scalar_tensor_tensor(
+                        out=sq[:, t, :], in0=z0[:], scalar=-2.0 * t, in1=sq[:, 0, :], op0=ALU.mult, op1=ALU.add,
+                    )
+                squares[a] = sq
+
+            def exp_step(a):
+                sq = squares[a]
+                e_planes = work.tile([P, PACK, BASIS_STEP], BF16, name="e_planes")
+                nc.scalar.activation(out=e_planes[:, 0:2, :], in_=sq[:, 0:2, :], func=ACT.Exp, scale=-WIDTH)
+                for t in range(2, PACK):
+                    nc.scalar.activation(
+                        out=e_planes[:, t, :], in_=sq[:, t, :], func=ACT.Exp, scale=-WIDTH, bias=exp_bias[:, t : t + 1],
+                    )
+                e_grouped = work.tile([P, BASIS_STEP, PACK], BF16, name="e_grouped", bufs=3, align_bytes=64)
+                nc.vector.tensor_copy(
+                    out=e_grouped[:].rearrange("p (c i) t -> p c t i", i=4),
+                    in_=e_planes[:].rearrange("p t (c i) -> p c t i", i=4),
+                )
+                grouped[a] = e_grouped
+
+            def quantise_step(a):
+                cols = slice(a * BASIS_STEP, (a + 1) * BASIS_STEP)
+                nc.vector.quantize_mx(
+                    out=moving_codes[HIDDEN][:, cols].bitcast(FP8X4),
+                    scales=moving_scales[HIDDEN][:, cols],
+                    in_=grouped[a][:].rearrange("p w t -> p (w t)"),
+                )
+
+            def basis_round(a):
+                if a < BASIS_STEPS:
+                    square_step(a)
+                if 1 <= a <= BASIS_STEPS:
+                    exp_step(a - 1)
+                if a >= 2:
+                    quantise_step(a - 2)
+
+            basis_round(0)
+            basis_round(1)
+            for layer, sign in enumerate((-1.0, 1.0)):
+                grouped_w = work.tile([P, PACK, P, PACK], BF16, name="grouped_w", align_bytes=64)
+                nc.gpsimd.tensor_scalar(
+                    out=grouped_w[:],
+                    in0=raw_weights[layer][:].rearrange("p j (c m) -> p m c j", m=PACK),
+                    scalar1=sign,
+                    scalar2=0.0,
+                    op0=ALU.mult,
+                    op1=ALU.add,
+                )
+                nc.vector.quantize_mx(
+                    out=weight_codes[layer][:].bitcast(FP8X4),
+                    scales=weight_scales[layer][:],
+                    in_=grouped_w[:].rearrange("p m c j -> p (m c j)"),
+                )
+                nc.vector.tensor_scalar(
+                    out=minus_bias[layer][:], in0=raw_biases[layer][:], scalar1=-1.0, scalar2=None, op0=ALU.mult,
+                )
+                nc.vector.tensor_scalar(
+                    out=guard_bias[layer][:], in0=raw_biases[layer][:], scalar1=-1.0, scalar2=LN2,
+                    op0=ALU.mult, op1=ALU.add,
+                )
+            for a in range(2, BASIS_STEPS + 2):
+                basis_round(a)
+
+        with tc.tile_pool(name="layers", bufs=2, reuse_waits="tile") as work:
+            x_all = work.tile([P, OUT_TILES, FEATURES], BF16, name="x_all", bufs=1)
+            nc.sync.dma_start(out=x_all[:], in_=x_rows.rearrange("(n p) f -> p n f", p=P))
+            minus_sum = work.tile([P, PACK, ATOM_ROWS], F32, name="minus_sum", bufs=1)
+
+            def multiply(layer, c, m, bank):
+                feats = slice(m * P, (m + 1) * P)
+                cols = slice(c * CHUNK, (c + 1) * CHUNK)
+                nc.tensor.matmul_mx(
+                    out=bank[:],
+                    lhsT=weight_codes[layer][:, feats].bitcast(FP8X4),
+                    lhsT_scale=weight_scales[layer][:, feats],
+                    rhs=moving_codes[layer][:, cols].bitcast(FP8X4),
+                    rhs_scale=moving_scales[layer][:, cols],
+                    start=True,
+                    stop=True,
+                )
+
+            def sigmoid_chunk(layer, c):
+                soft = work.tile([P, PACK, CHUNK], F32, name="soft", bufs=9)
+                for m in range(PACK):
+                    bank = psum.tile([P, CHUNK], F32, name="bank_s", tag="for_scalar")
+                    multiply(layer, c, m, bank)
+                    nc.scalar.activation(
+                        out=soft[:, m, :], in_=bank[:], func=ACT.Sigmoid, bias=minus_bias[layer][:, m : m + 1],
+                    )
+                return soft
+
+            def log_chunk(soft):
+                nc.scalar.activation(out=soft[:], in_=soft[:], func=ACT.Ln, scale=2.0, bias=tiny[:])
+
+            def guard_chunk(layer, c, soft, result):
+                for m in range(PACK):
+                    bank = psum.tile([P, CHUNK], F32, name="bank_v", tag="for_vector")
+                    multiply(layer, c, m, bank)
+                    nc.vector.scalar_tensor_tensor(
+                        out=result[:, m, :], in0=bank[:], scalar=guard_bias[layer][:, m : m + 1], in1=soft[:, m, :],
+                        op0=ALU.add, op1=ALU.min,
+                    )
+
+            def regroup_hidden(c, soft):
+                h_planes = work.tile([P, PACK, CHUNK], BF16, name="h_planes")
+                guard_chunk(HIDDEN, c, soft, h_planes)
+                h_grouped = work.tile([P, CHUNK, PACK], BF16, name="h_grouped", bufs=3, align_bytes=64)
+                nc.vector.tensor_copy(
+                    out=h_grouped[:].rearrange("p (c i) t -> p c t i", i=4),
+                    in_=h_planes[:].rearrange("p t (c i) -> p c t i", i=4),
+                )
+                return h_grouped
+
+            def quantise_hidden(c, h_grouped):
+                cols = slice(c * CHUNK, (c + 1) * CHUNK)
+                nc.vector.quantize_mx(
+                    out=moving_codes[FILTER][:, cols].bitcast(FP8X4),
+                    scales=moving_scales[FILTER][:, cols],
+                    in_=h_grouped[:].rearrange("p w t -> p (w t)"),
+                )
+
+            def finish_filter(c, soft):
+                guard_chunk(FILTER, c, soft, soft)
+                rows = slice(c * CHUNK // ATOMS, (c + 1) * CHUNK // ATOMS)
+                eight = soft[:].rearrange("p m (q two) -> p (m q) two", two=2)
+                four = work.tile([P, PACK * CHUNK // 2], F32, name="four", bufs=1)
+                nc.gpsimd.tensor_tensor(out=four[:], in0=eight[:, :, 0], in1=eight[:, :, 1], op=ALU.add)
+                four_pairs = four[:].rearrange("p (q two) -> p q two", two=2)
+                two = work.tile([P, PACK * CHUNK // 4], F32, name="two", bufs=1)
+                nc.gpsimd.tensor_tensor(out=two[:], in0=four_pairs[:, :, 0], in1=four_pairs[:, :, 1], op=ALU.add)
+                two_pairs = two[:].rearrange("p (m a two) -> p m a two", m=PACK, two=2)
+                nc.gpsimd.tensor_tensor(
+                    out=minus_sum[:, :, rows], in0=two_pairs[:, :, :, 0], in1=two_pairs[:, :, :, 1], op=ALU.add,
+                )
+                if (c + 1) % CHUNKS_PER_OUT_TILE == 0:
+                    store_out_tile(c // CHUNKS_PER_OUT_TILE)
+
+            def store_out_tile(n):
+                rows = slice(n * P, (n + 1) * P)
+                turned = psum.tile([P, PACK, P], F32, name="turned", tag="for_vector")
+                for m in range(PACK):
+                    nc.tensor.transpose(turned[:, m, :], minus_sum[:, m, rows], identity[:])
+                product = work.tile([P, FEATURES], F32, name="product")
+                nc.vector.scalar_tensor_tensor(
+                    out=product[:].rearrange("p (c m) -> p c m", m=PACK),
+                    in0=turned[:].rearrange("p m c -> p c m"),
+                    scalar=-1.0,
+                    in1=x_all[:, n, :].rearrange("p (c m) -> p c m", m=PACK),
+                    op0=ALU.mult,
+                    op1=ALU.mult,
+                )
+                nc.sync.dma_start(out=out_rows[rows, :], in_=product[:])
+
+            waiting = []
+            for r in range(BATCHES + 1):
+                units = []
+                if r < BATCHES:
+                    units.extend([(HIDDEN, c) for c in range(r * BATCH, (r + 1) * BATCH)])
+                if r >= 1:
+                    units.extend([(FILTER, c) for c in range((r - 1) * BATCH, r * BATCH)])
+                softs = []
+                for i, (layer, c) in enumerate(units):
+                    softs.append(sigmoid_chunk(layer, c))
+                    if i < len(waiting):
+                        finish_filter(*waiting[i])
+                for soft in softs:
+                    log_chunk(soft)
+                waiting = []
+                previous = None
+                for (layer, c), soft in zip(units, softs):
+                    if layer == HIDDEN:
+                        h_grouped = regroup_hidden(c, soft)
+                        if previous is not None:
+                            quantise_hidden(*previous)
+                        previous = (c, h_grouped)
+                    else:
+                        waiting.append((c, soft))
+                if previous is not None:
+                    quantise_hidden(*previous)
+            for c, soft in waiting:
+                finish_filter(c, soft)

@@ -69,11 +69,11 @@ def tile_cfconv_pa_t_kernel(tc, x, distances, W1, b1, W2, b2, out):
         nc.vector.tensor_copy(out=centre[:], in_=centre_int[:])
         minus_centre = keep.tile([P, PACK], F32, name="minus_centre")
         nc.vector.tensor_scalar(out=minus_centre[:], in0=centre[:], scalar1=-1.0, scalar2=None, op0=ALU.mult)
-        t_squared = keep.tile([P, PACK], F32, name="t_squared")
+        whole = keep.tile([P, PACK], F32, name="whole")
         for t in range(PACK):
-            nc.vector.memset(t_squared[:, t : t + 1], float(t * t))
+            nc.vector.memset(whole[:, t : t + 1], float(t * (t - 1)))
         exp_bias = keep.tile([P, PACK], F32, name="exp_bias")
-        nc.vector.tensor_scalar(out=exp_bias[:], in0=t_squared[:], scalar1=-WIDTH, scalar2=None, op0=ALU.mult)
+        nc.vector.tensor_scalar(out=exp_bias[:], in0=whole[:], scalar1=-WIDTH, scalar2=None, op0=ALU.mult)
         tiny = keep.tile([P, 1], F32, name="tiny")
         nc.vector.memset(tiny[:], TINY)
         identity = keep.tile([P, P], F32, name="identity")
@@ -104,7 +104,6 @@ def tile_cfconv_pa_t_kernel(tc, x, distances, W1, b1, W2, b2, out):
                 load_distances(a)
 
             squares = {}
-            planes = {}
             grouped = {}
 
             def square_step(a):
@@ -115,14 +114,10 @@ def tile_cfconv_pa_t_kernel(tc, x, distances, W1, b1, W2, b2, out):
                         out=sq[:, t, :], in_=d_all[:, cols], func=ACT.Square,
                         scale=INV_STEP, bias=minus_centre[:, t : t + 1],
                     )
-                z0 = work.tile([P, BASIS_STEP], F32, name="z0")
-                nc.gpsimd.tensor_scalar(
-                    out=z0[:], in0=d_all[:, cols], scalar1=INV_STEP, scalar2=centre[:, 0:1],
-                    op0=ALU.mult, op1=ALU.subtract,
-                )
                 for t in range(2, PACK):
                     nc.vector.scalar_tensor_tensor(
-                        out=sq[:, t, :], in0=z0[:], scalar=-2.0 * t, in1=sq[:, 0, :], op0=ALU.mult, op1=ALU.add,
+                        out=sq[:, t, :], in0=sq[:, 1, :], scalar=t / (t - 1.0), in1=sq[:, 0, :],
+                        op0=ALU.mult, op1=ALU.subtract,
                     )
                 squares[a] = sq
 
@@ -132,7 +127,8 @@ def tile_cfconv_pa_t_kernel(tc, x, distances, W1, b1, W2, b2, out):
                 nc.scalar.activation(out=e_planes[:, 0:2, :], in_=sq[:, 0:2, :], func=ACT.Exp, scale=-WIDTH)
                 for t in range(2, PACK):
                     nc.scalar.activation(
-                        out=e_planes[:, t, :], in_=sq[:, t, :], func=ACT.Exp, scale=-WIDTH, bias=exp_bias[:, t : t + 1],
+                        out=e_planes[:, t, :], in_=sq[:, t, :], func=ACT.Exp,
+                        scale=-WIDTH * (t - 1), bias=exp_bias[:, t : t + 1],
                     )
                 e_grouped = work.tile([P, BASIS_STEP, PACK], BF16, name="e_grouped", bufs=3, align_bytes=64)
                 nc.vector.tensor_copy(
@@ -224,10 +220,8 @@ def tile_cfconv_pa_t_kernel(tc, x, distances, W1, b1, W2, b2, out):
                         op0=ALU.add, op1=ALU.min,
                     )
 
-            def regroup_hidden(c, soft):
-                h_planes = work.tile([P, PACK, CHUNK], BF16, name="h_planes")
-                guard_chunk(HIDDEN, c, soft, h_planes)
-                h_grouped = work.tile([P, CHUNK, PACK], BF16, name="h_grouped", bufs=3, align_bytes=64)
+            def regroup_hidden(h_planes):
+                h_grouped = work.tile([P, CHUNK, PACK], BF16, name="h_grouped", bufs=BATCH, align_bytes=64)
                 nc.vector.tensor_copy(
                     out=h_grouped[:].rearrange("p (c i) t -> p c t i", i=4),
                     in_=h_planes[:].rearrange("p t (c i) -> p c t i", i=4),
@@ -242,21 +236,14 @@ def tile_cfconv_pa_t_kernel(tc, x, distances, W1, b1, W2, b2, out):
                     in_=h_grouped[:].rearrange("p w t -> p (w t)"),
                 )
 
-            def finish_filter(c, soft):
-                guard_chunk(FILTER, c, soft, soft)
+            def sum_neighbours(c, soft):
                 rows = slice(c * CHUNK // ATOMS, (c + 1) * CHUNK // ATOMS)
-                eight = soft[:].rearrange("p m (q two) -> p (m q) two", two=2)
-                four = work.tile([P, PACK * CHUNK // 2], F32, name="four", bufs=1)
-                nc.gpsimd.tensor_tensor(out=four[:], in0=eight[:, :, 0], in1=eight[:, :, 1], op=ALU.add)
-                four_pairs = four[:].rearrange("p (q two) -> p q two", two=2)
-                two = work.tile([P, PACK * CHUNK // 4], F32, name="two", bufs=1)
-                nc.gpsimd.tensor_tensor(out=two[:], in0=four_pairs[:, :, 0], in1=four_pairs[:, :, 1], op=ALU.add)
-                two_pairs = two[:].rearrange("p (m a two) -> p m a two", m=PACK, two=2)
-                nc.gpsimd.tensor_tensor(
-                    out=minus_sum[:, :, rows], in0=two_pairs[:, :, :, 0], in1=two_pairs[:, :, :, 1], op=ALU.add,
+                nc.vector.tensor_reduce(
+                    out=minus_sum[:, :, rows],
+                    in_=soft[:].rearrange("p m (a j) -> p m a j", j=ATOMS),
+                    axis=mybir.AxisListType.X,
+                    op=ALU.add,
                 )
-                if (c + 1) % CHUNKS_PER_OUT_TILE == 0:
-                    store_out_tile(c // CHUNKS_PER_OUT_TILE)
 
             def store_out_tile(n):
                 rows = slice(n * P, (n + 1) * P)
@@ -274,31 +261,31 @@ def tile_cfconv_pa_t_kernel(tc, x, distances, W1, b1, W2, b2, out):
                 )
                 nc.sync.dma_start(out=out_rows[rows, :], in_=product[:])
 
-            waiting = []
-            for r in range(BATCHES + 1):
+            guarded_hidden = []
+            guarded_filter = []
+            for r in range(BATCHES + 2):
+                regrouped = [(c, regroup_hidden(h_planes)) for c, h_planes in guarded_hidden]
+                for c, h_grouped in regrouped:
+                    quantise_hidden(c, h_grouped)
+                for c, soft in guarded_filter:
+                    sum_neighbours(c, soft)
                 units = []
                 if r < BATCHES:
                     units.extend([(HIDDEN, c) for c in range(r * BATCH, (r + 1) * BATCH)])
-                if r >= 1:
+                if 1 <= r <= BATCHES:
                     units.extend([(FILTER, c) for c in range((r - 1) * BATCH, r * BATCH)])
-                softs = []
-                for i, (layer, c) in enumerate(units):
-                    softs.append(sigmoid_chunk(layer, c))
-                    if i < len(waiting):
-                        finish_filter(*waiting[i])
-                for soft in softs:
-                    log_chunk(soft)
-                waiting = []
-                previous = None
+                softs = [sigmoid_chunk(layer, c) for layer, c in units]
+                for c, soft in guarded_filter:
+                    if (c + 1) % CHUNKS_PER_OUT_TILE == 0:
+                        store_out_tile(c // CHUNKS_PER_OUT_TILE)
+                guarded_hidden = []
+                guarded_filter = []
                 for (layer, c), soft in zip(units, softs):
+                    log_chunk(soft)
                     if layer == HIDDEN:
-                        h_grouped = regroup_hidden(c, soft)
-                        if previous is not None:
-                            quantise_hidden(*previous)
-                        previous = (c, h_grouped)
+                        h_planes = work.tile([P, PACK, CHUNK], BF16, name="h_planes", bufs=BATCH + 1)
+                        guard_chunk(HIDDEN, c, soft, h_planes)
+                        guarded_hidden.append((c, h_planes))
                     else:
-                        waiting.append((c, soft))
-                if previous is not None:
-                    quantise_hidden(*previous)
-            for c, soft in waiting:
-                finish_filter(c, soft)
+                        guard_chunk(FILTER, c, soft, soft)
+                        guarded_filter.append((c, soft))

@@ -28,8 +28,8 @@ BASIS_STEP = 1024
 BASIS_STEPS = PAIRS // BASIS_STEP
 CHUNK = 512
 CHUNKS = PAIRS // CHUNK
-BATCH = 3
-BATCHES = CHUNKS // BATCH
+BATCH = 5
+BATCHES = (CHUNKS + BATCH - 1) // BATCH
 OUT_TILES = ATOM_ROWS // P
 CHUNKS_PER_OUT_TILE = P * ATOMS // CHUNK
 
@@ -46,14 +46,8 @@ def tile_cfconv_pa_t_kernel(tc, x, distances, W1, b1, W2, b2, out):
     out_rows = out.rearrange("b i f -> (b i) f")
 
     with tc.manual_schedule(), tc.tile_pool(name="keep", bufs=1) as keep, tc.psum_pool(name="psum", bufs=4) as psum:
-        moving_codes = [
-            keep.tile([P, PAIRS], U32, name="basis_codes", align_bytes=64),
-            keep.tile([P, PAIRS], U32, name="hidden_codes", align_bytes=64),
-        ]
-        moving_scales = [
-            keep.tile([P, PAIRS], U8, name="basis_scales", align_bytes=64),
-            keep.tile([P, PAIRS], U8, name="hidden_scales", align_bytes=64),
-        ]
+        moving_codes = keep.tile([P, PAIRS], U32, name="moving_codes", align_bytes=64)
+        moving_scales = keep.tile([P, PAIRS], U8, name="moving_scales", align_bytes=64)
         weight_codes = [
             keep.tile([P, FEATURES], U32, name="w1_codes", align_bytes=64),
             keep.tile([P, FEATURES], U32, name="w2_codes", align_bytes=64),
@@ -140,8 +134,8 @@ def tile_cfconv_pa_t_kernel(tc, x, distances, W1, b1, W2, b2, out):
             def quantise_step(a):
                 cols = slice(a * BASIS_STEP, (a + 1) * BASIS_STEP)
                 nc.vector.quantize_mx(
-                    out=moving_codes[HIDDEN][:, cols].bitcast(FP8X4),
-                    scales=moving_scales[HIDDEN][:, cols],
+                    out=moving_codes[:, cols].bitcast(FP8X4),
+                    scales=moving_scales[:, cols],
                     in_=grouped[a][:].rearrange("p w t -> p (w t)"),
                 )
 
@@ -192,19 +186,25 @@ def tile_cfconv_pa_t_kernel(tc, x, distances, W1, b1, W2, b2, out):
                     out=bank[:],
                     lhsT=weight_codes[layer][:, feats].bitcast(FP8X4),
                     lhsT_scale=weight_scales[layer][:, feats],
-                    rhs=moving_codes[layer][:, cols].bitcast(FP8X4),
-                    rhs_scale=moving_scales[layer][:, cols],
+                    rhs=moving_codes[:, cols].bitcast(FP8X4),
+                    rhs_scale=moving_scales[:, cols],
                     start=True,
                     stop=True,
                 )
 
-            def sigmoid_chunk(layer, c):
-                soft = work.tile([P, PACK, CHUNK], F32, name="soft", bufs=9)
+            def products_for_scalar(layer, c):
+                banks = []
                 for m in range(PACK):
                     bank = psum.tile([P, CHUNK], F32, name="bank_s", tag="for_scalar")
                     multiply(layer, c, m, bank)
+                    banks.append(bank)
+                return banks
+
+            def sigmoid_chunk(layer, banks):
+                soft = work.tile([P, PACK, CHUNK], F32, name="soft", bufs=2 * BATCH + 2)
+                for m in range(PACK):
                     nc.scalar.activation(
-                        out=soft[:, m, :], in_=bank[:], func=ACT.Sigmoid, bias=minus_bias[layer][:, m : m + 1],
+                        out=soft[:, m, :], in_=banks[m][:], func=ACT.Sigmoid, bias=minus_bias[layer][:, m : m + 1],
                     )
                 return soft
 
@@ -221,7 +221,7 @@ def tile_cfconv_pa_t_kernel(tc, x, distances, W1, b1, W2, b2, out):
                     )
 
             def regroup_hidden(h_planes):
-                h_grouped = work.tile([P, CHUNK, PACK], BF16, name="h_grouped", bufs=BATCH, align_bytes=64)
+                h_grouped = work.tile([P, CHUNK, PACK], BF16, name="h_grouped", bufs=3, align_bytes=64)
                 nc.vector.tensor_copy(
                     out=h_grouped[:].rearrange("p (c i) t -> p c t i", i=4),
                     in_=h_planes[:].rearrange("p t (c i) -> p c t i", i=4),
@@ -231,8 +231,8 @@ def tile_cfconv_pa_t_kernel(tc, x, distances, W1, b1, W2, b2, out):
             def quantise_hidden(c, h_grouped):
                 cols = slice(c * CHUNK, (c + 1) * CHUNK)
                 nc.vector.quantize_mx(
-                    out=moving_codes[FILTER][:, cols].bitcast(FP8X4),
-                    scales=moving_scales[FILTER][:, cols],
+                    out=moving_codes[:, cols].bitcast(FP8X4),
+                    scales=moving_scales[:, cols],
                     in_=h_grouped[:].rearrange("p w t -> p (w t)"),
                 )
 
@@ -261,23 +261,32 @@ def tile_cfconv_pa_t_kernel(tc, x, distances, W1, b1, W2, b2, out):
                 )
                 nc.sync.dma_start(out=out_rows[rows, :], in_=product[:])
 
+            def chunks_of_batch(b):
+                return range(b * BATCH, min((b + 1) * BATCH, CHUNKS))
+
             guarded_hidden = []
             guarded_filter = []
+            early_banks = products_for_scalar(HIDDEN, 0)
             for r in range(BATCHES + 2):
-                regrouped = [(c, regroup_hidden(h_planes)) for c, h_planes in guarded_hidden]
-                for c, h_grouped in regrouped:
-                    quantise_hidden(c, h_grouped)
+                for c, h_planes in guarded_hidden:
+                    quantise_hidden(c, regroup_hidden(h_planes))
                 for c, soft in guarded_filter:
                     sum_neighbours(c, soft)
                 units = []
                 if r < BATCHES:
-                    units.extend([(HIDDEN, c) for c in range(r * BATCH, (r + 1) * BATCH)])
+                    units.extend([(HIDDEN, c) for c in chunks_of_batch(r)])
                 if 1 <= r <= BATCHES:
-                    units.extend([(FILTER, c) for c in range((r - 1) * BATCH, r * BATCH)])
-                softs = [sigmoid_chunk(layer, c) for layer, c in units]
+                    units.extend([(FILTER, c) for c in chunks_of_batch(r - 1)])
+                softs = []
+                for layer, c in units:
+                    banks = early_banks if early_banks is not None else products_for_scalar(layer, c)
+                    early_banks = None
+                    softs.append(sigmoid_chunk(layer, banks))
                 for c, soft in guarded_filter:
                     if (c + 1) % CHUNKS_PER_OUT_TILE == 0:
                         store_out_tile(c // CHUNKS_PER_OUT_TILE)
+                if r + 1 < BATCHES:
+                    early_banks = products_for_scalar(HIDDEN, (r + 1) * BATCH)
                 guarded_hidden = []
                 guarded_filter = []
                 for (layer, c), soft in zip(units, softs):

@@ -18,20 +18,29 @@ ATOMS = 8
 ATOM_ROWS = 144 * ATOMS
 PAIRS = ATOM_ROWS * ATOMS
 FEATURES = P * PACK
+TILES = ATOM_ROWS // P
 
 INV_STEP = 10.0
 WIDTH = 0.1
 LN2 = math.log(2.0)
 TINY = 2.0**-62
+CAP = 12.0
+FLOOR = 1.0 / (1.0 + math.exp(CAP))
+LOG_SCALE = 64.0
 
-BASIS_STEP = 1024
-BASIS_STEPS = PAIRS // BASIS_STEP
+BLOCK = P
 CHUNK = 512
+BLOCKS = CHUNK // BLOCK
 CHUNKS = PAIRS // CHUNK
-BATCH = 5
-BATCHES = (CHUNKS + BATCH - 1) // BATCH
-OUT_TILES = ATOM_ROWS // P
-CHUNKS_PER_OUT_TILE = P * ATOMS // CHUNK
+UNITS = [(0, 2), (2, 2), (4, 2), (6, 2), (8, 1)]
+BATCHES = [4, 5, 5, 4]
+PLANE_CHUNKS = 4
+ROWS = 8
+GROUPS = P // ROWS
+SPREADS = 4
+AHEAD = 4
+SOFTS = 9
+LATE = [4]
 
 HIDDEN = 0
 FILTER = 1
@@ -41,24 +50,41 @@ FLOPS = 2 * 2 * PAIRS * FEATURES * FEATURES
 
 def tile_cfconv_pa_t_kernel(tc, x, distances, W1, b1, W2, b2, out):
     nc = tc.nc
-    d_flat = distances.rearrange("b i j -> (b i j)")
-    x_rows = x.rearrange("b i f -> (b i) f")
-    out_rows = out.rearrange("b i f -> (b i) f")
+    x_rows = x.rearrange("b i f -> (b i) f").rearrange("(q n) f -> q n f", n=TILES)
+    out_rows = out.rearrange("b i f -> (b i) f").rearrange("(q n) f -> q n f", n=TILES)
+    d_rows = distances.rearrange("b i j -> (b i) j").rearrange("(q n) j -> q n j", n=TILES)
 
-    with tc.manual_schedule(), tc.tile_pool(name="keep", bufs=1) as keep, tc.psum_pool(name="psum", bufs=4) as psum:
-        moving_codes = keep.tile([P, PAIRS], U32, name="moving_codes", align_bytes=64)
-        moving_scales = keep.tile([P, PAIRS], U8, name="moving_scales", align_bytes=64)
-        weight_codes = [
-            keep.tile([P, FEATURES], U32, name="w1_codes", align_bytes=64),
-            keep.tile([P, FEATURES], U32, name="w2_codes", align_bytes=64),
-        ]
-        weight_scales = [
-            keep.tile([P, FEATURES], U8, name="w1_scales", align_bytes=64),
-            keep.tile([P, FEATURES], U8, name="w2_scales", align_bytes=64),
-        ]
+    chunk_unit = []
+    chunk_blocks = []
+    for u, (first, width) in enumerate(UNITS):
+        slots = BLOCKS // width
+        for k in range(ATOMS // slots):
+            chunk_unit.append((u, k))
+            chunk_blocks.append([(first + w, k * slots + s) for s in range(slots) for w in range(width)])
 
+    with tc.manual_schedule(), tc.tile_pool(name="keep", bufs=1) as keep, tc.tile_pool(
+        name="work", bufs=2, reuse_waits="tile"
+    ) as work, tc.psum_pool(name="psum", bufs=4) as psum:
+        d_raw = keep.tile([P, TILES, ATOMS], BF16, name="d_raw")
+        nc.sync.dma_start(out=d_raw[:], in_=d_rows)
+        raw_weights = []
+        raw_biases = []
+        for layer, (weight, bias) in enumerate(((W1, b1), (W2, b2))):
+            raw_w = work.tile([P, PACK, FEATURES], BF16, name="raw_w", tag="soft", bufs=SOFTS)
+            nc.sync.dma_start(out=raw_w[:], in_=weight.rearrange("(p j) f -> p j f", j=PACK))
+            raw_weights.append(raw_w)
+            raw_b = keep.tile([P, PACK], BF16, name="raw_b%d" % layer)
+            nc.sync.dma_start(out=raw_b[:], in_=bias.rearrange("(c m) -> c m", m=PACK))
+            raw_biases.append(raw_b)
+        x_all = keep.tile([P, TILES, FEATURES], BF16, name="x_all")
+        nc.sync.dma_start(out=x_all[:], in_=x_rows)
+
+        identity_b = keep.tile([P, P], BF16, name="identity_b")
+        make_identity(nc, identity_b[:])
         centre_int = keep.tile([P, PACK], I32, name="centre_int")
         nc.gpsimd.iota(centre_int[:], pattern=[[1, PACK]], base=0, channel_multiplier=PACK)
+        identity = keep.tile([P, P], F32, name="identity")
+        make_identity(nc, identity[:])
         centre = keep.tile([P, PACK], F32, name="centre")
         nc.vector.tensor_copy(out=centre[:], in_=centre_int[:])
         minus_centre = keep.tile([P, PACK], F32, name="minus_centre")
@@ -70,231 +96,513 @@ def tile_cfconv_pa_t_kernel(tc, x, distances, W1, b1, W2, b2, out):
         nc.vector.tensor_scalar(out=exp_bias[:], in0=whole[:], scalar1=-WIDTH, scalar2=None, op0=ALU.mult)
         tiny = keep.tile([P, 1], F32, name="tiny")
         nc.vector.memset(tiny[:], TINY)
-        identity = keep.tile([P, P], F32, name="identity")
-        make_identity(nc, identity[:])
 
+        moving_codes = keep.tile([P, PAIRS], U32, name="moving_codes", align_bytes=64)
+        moving_scales = keep.tile([P, PAIRS], U8, name="moving_scales", align_bytes=64)
+        weight_codes = [
+            keep.tile([P, FEATURES], U32, name="w1_codes", align_bytes=64),
+            keep.tile([P, FEATURES], U32, name="w2_codes", align_bytes=64),
+        ]
+        weight_scales = [
+            keep.tile([P, FEATURES], U8, name="w1_scales", align_bytes=64),
+            keep.tile([P, FEATURES], U8, name="w2_scales", align_bytes=64),
+        ]
         minus_bias = [keep.tile([P, PACK], F32, name="minus_b1"), keep.tile([P, PACK], F32, name="minus_b2")]
-        guard_bias = [keep.tile([P, PACK], F32, name="guard_b1"), keep.tile([P, PACK], F32, name="guard_b2")]
+        guard_bias = keep.tile([P, PACK], F32, name="guard_bias")
+        guard_bias2 = keep.tile([P, PACK], F32, name="guard_bias2")
+        limit = keep.tile([P, PACK], F32, name="limit")
+        offset = {1: keep.tile([P, PACK], F32, name="offset1"), 2: keep.tile([P, PACK], F32, name="offset2")}
 
-        with tc.tile_pool(name="basis", bufs=2) as work:
-            d_all = work.tile([P, PAIRS], BF16, name="d_all", bufs=1)
+        def quantise_columns(cols, grouped):
+            nc.vector.quantize_mx(
+                out=moving_codes[:, cols].bitcast(FP8X4),
+                scales=moving_scales[:, cols],
+                in_=grouped[:].rearrange("p w t -> p (w t)"),
+            )
 
-            def load_distances(a):
-                cols = slice(a * BASIS_STEP, (a + 1) * BASIS_STEP)
-                nc.sync.dma_start(out=d_all[:, cols], in_=d_flat[cols].partition_broadcast(P))
+        def chunk_cols(c):
+            return slice(c * CHUNK, (c + 1) * CHUNK)
 
-            load_distances(0)
-            load_distances(1)
-            raw_weights = []
-            raw_biases = []
-            for layer, (weight, bias) in enumerate(((W1, b1), (W2, b2))):
-                raw_w = work.tile([P, PACK, FEATURES], BF16, name="raw_w")
-                nc.sync.dma_start(out=raw_w[:], in_=weight.rearrange("(p j) f -> p j f", j=PACK))
-                raw_weights.append(raw_w)
-                raw_b = work.tile([P, PACK], BF16, name="raw_b")
-                nc.sync.dma_start(out=raw_b[:], in_=bias.rearrange("(c m) -> c m", m=PACK))
-                raw_biases.append(raw_b)
-            for a in range(2, BASIS_STEPS):
-                load_distances(a)
+        def prepare_layer(layer):
+            sign = -1.0 if layer == HIDDEN else 1.0
+            grouped_w = work.tile([P, PACK, P, PACK], BF16, name="grouped_w", tag="grouped", bufs=4, align_bytes=64)
+            nc.gpsimd.tensor_scalar(
+                out=grouped_w[:],
+                in0=raw_weights[layer][:].rearrange("p j (c m) -> p m c j", m=PACK),
+                scalar1=sign,
+                scalar2=0.0,
+                op0=ALU.mult,
+                op1=ALU.add,
+            )
+            nc.vector.quantize_mx(
+                out=weight_codes[layer][:].bitcast(FP8X4),
+                scales=weight_scales[layer][:],
+                in_=grouped_w[:].rearrange("p m c j -> p (m c j)"),
+            )
+            nc.vector.tensor_scalar(
+                out=minus_bias[layer][:], in0=raw_biases[layer][:], scalar1=-1.0, scalar2=None, op0=ALU.mult
+            )
 
-            squares = {}
-            grouped = {}
-
-            def square_step(a):
-                cols = slice(a * BASIS_STEP, (a + 1) * BASIS_STEP)
-                sq = work.tile([P, PACK, BASIS_STEP], F32, name="sq")
-                for t in range(2):
-                    nc.scalar.activation(
-                        out=sq[:, t, :], in_=d_all[:, cols], func=ACT.Square,
-                        scale=INV_STEP, bias=minus_centre[:, t : t + 1],
-                    )
-                for t in range(2, PACK):
-                    nc.vector.scalar_tensor_tensor(
-                        out=sq[:, t, :], in0=sq[:, 1, :], scalar=t / (t - 1.0), in1=sq[:, 0, :],
-                        op0=ALU.mult, op1=ALU.subtract,
-                    )
-                squares[a] = sq
-
-            def exp_step(a):
-                sq = squares[a]
-                e_planes = work.tile([P, PACK, BASIS_STEP], BF16, name="e_planes")
-                nc.scalar.activation(out=e_planes[:, 0:2, :], in_=sq[:, 0:2, :], func=ACT.Exp, scale=-WIDTH)
-                for t in range(2, PACK):
-                    nc.scalar.activation(
-                        out=e_planes[:, t, :], in_=sq[:, t, :], func=ACT.Exp,
-                        scale=-WIDTH * (t - 1), bias=exp_bias[:, t : t + 1],
-                    )
-                e_grouped = work.tile([P, BASIS_STEP, PACK], BF16, name="e_grouped", bufs=3, align_bytes=64)
-                nc.vector.tensor_copy(
-                    out=e_grouped[:].rearrange("p (c i) t -> p c t i", i=4),
-                    in_=e_planes[:].rearrange("p t (c i) -> p c t i", i=4),
-                )
-                grouped[a] = e_grouped
-
-            def quantise_step(a):
-                cols = slice(a * BASIS_STEP, (a + 1) * BASIS_STEP)
-                nc.vector.quantize_mx(
-                    out=moving_codes[:, cols].bitcast(FP8X4),
-                    scales=moving_scales[:, cols],
-                    in_=grouped[a][:].rearrange("p w t -> p (w t)"),
+        def prepare_biases():
+            nc.vector.tensor_scalar(
+                out=guard_bias[:], in0=raw_biases[HIDDEN][:], scalar1=-1.0, scalar2=LN2, op0=ALU.mult, op1=ALU.add
+            )
+            nc.vector.tensor_scalar(
+                out=guard_bias2[:], in0=raw_biases[FILTER][:], scalar1=-1.0, scalar2=LN2, op0=ALU.mult, op1=ALU.add
+            )
+            nc.vector.tensor_scalar(
+                out=limit[:], in0=raw_biases[FILTER][:], scalar1=-CAP, scalar2=None, op0=ALU.add
+            )
+            for width in (1, 2):
+                steps = ATOMS * width // BLOCKS
+                nc.vector.tensor_scalar(
+                    out=offset[width][:], in0=raw_biases[FILTER][:], scalar1=-float(steps),
+                    scalar2=steps * (CAP + LN2) - math.log(LOG_SCALE), op0=ALU.mult, op1=ALU.add,
                 )
 
-            def basis_round(a):
-                if a < BASIS_STEPS:
-                    square_step(a)
-                if 1 <= a <= BASIS_STEPS:
-                    exp_step(a - 1)
-                if a >= 2:
-                    quantise_step(a - 2)
+        squares = {}
+        spreads = {}
+        planes = {}
 
-            basis_round(0)
-            basis_round(1)
-            for layer, sign in enumerate((-1.0, 1.0)):
-                grouped_w = work.tile([P, PACK, P, PACK], BF16, name="grouped_w", align_bytes=64)
+        def square_chunk(c):
+            spread = psum.tile([P, CHUNK], BF16, name="spread", tag="for_scalar")
+            for i, (n, j) in enumerate(chunk_blocks[c]):
+                nc.tensor.transpose(
+                    spread[:, i * BLOCK : (i + 1) * BLOCK],
+                    d_raw[:, n, j : j + 1].to_broadcast([P, P]),
+                    identity_b[:],
+                )
+            spreads[c] = spread
+
+        def square_acts(c):
+            spread = spreads[c]
+            sq = work.tile([P, PACK, CHUNK], F32, name="sq", tag="soft", bufs=SOFTS)
+            for t in range(2):
+                nc.scalar.activation(
+                    out=sq[:, t, :], in_=spread[:], func=ACT.Square, scale=INV_STEP, bias=minus_centre[:, t : t + 1]
+                )
+            for t in range(2, PACK):
+                nc.vector.scalar_tensor_tensor(
+                    out=sq[:, t, :], in0=sq[:, 1, :], scalar=t / (t - 1.0), in1=sq[:, 0, :],
+                    op0=ALU.mult, op1=ALU.subtract,
+                )
+            squares[c] = sq
+
+        def exp_chunk(c):
+            sq = squares[c]
+            e_planes = work.tile([P, PACK, CHUNK], BF16, name="e_planes", tag="planes", bufs=2)
+            nc.scalar.activation(out=e_planes[:, 0:2, :], in_=sq[:, 0:2, :], func=ACT.Exp, scale=-WIDTH)
+            for t in range(2, PACK):
+                nc.scalar.activation(
+                    out=e_planes[:, t, :], in_=sq[:, t, :], func=ACT.Exp,
+                    scale=-WIDTH * (t - 1), bias=exp_bias[:, t : t + 1],
+                )
+            planes[c] = e_planes
+
+        def regroup(source):
+            grouped = work.tile([P, CHUNK, PACK], BF16, name="grouped", bufs=4, align_bytes=64)
+            nc.vector.tensor_copy(
+                out=grouped[:].rearrange("p (c i) t -> p c t i", i=4),
+                in_=source[:].rearrange("p t (c i) -> p c t i", i=4),
+            )
+            return grouped
+
+        select = keep.tile([P, GROUPS, P], BF16, name="select")
+        features = keep.tile([P, SPREADS, CHUNK], BF16, name="features")
+
+        def prepare_select():
+            wcol = keep.tile([P, P], BF16, name="wcol")
+            w32 = keep.tile([P, 2], F32, name="w32")
+            nc.vector.memset(wcol[:, 0:3], 1.0)
+            nc.vector.tensor_scalar(out=w32[:, 0:1], in0=centre[:, 0:1], scalar1=-20.0, scalar2=None, op0=ALU.mult)
+            nc.vector.tensor_tensor(out=w32[:, 1:2], in0=centre[:, 0:1], in1=centre[:, 0:1], op=ALU.mult)
+            nc.vector.tensor_copy(out=wcol[:, 3:4], in_=w32[:, 0:1])
+            nc.vector.tensor_copy(out=wcol[:, 6:7], in_=w32[:, 1:2])
+            nc.vector.tensor_scalar(out=wcol[:, 5:6], in0=centre[:, 0:1], scalar1=2.0, scalar2=None, op0=ALU.mult)
+            nc.vector.tensor_tensor(out=wcol[:, 4:5], in0=w32[:, 0:1], in1=wcol[:, 3:4], op=ALU.subtract)
+            nc.vector.tensor_tensor(out=wcol[:, 7:8], in0=w32[:, 1:2], in1=wcol[:, 6:7], op=ALU.subtract)
+            have = ROWS
+            while have < P:
+                nc.vector.tensor_copy(out=wcol[:, have : 2 * have], in_=wcol[:, 0:have])
+                have *= 2
+            member = keep.tile([P, GROUPS], F32, name="member")
+            nc.vector.tensor_reduce(
+                out=member[:], in_=identity[:].rearrange("p (g r) -> p g r", r=ROWS), axis=mybir.AxisListType.X, op=ALU.add
+            )
+            turned = psum.tile([P, P], BF16, name="turned_w", tag="for_vector")
+            nc.tensor.transpose(turned[:], wcol[:], identity_b[:])
+            wrow = keep.tile([P, P], BF16, name="wrow")
+            nc.vector.tensor_copy(out=wrow[:], in_=turned[:])
+            return wrow, member
+
+        def fill_select(wrow, member):
+            for g in range(GROUPS):
                 nc.gpsimd.tensor_scalar(
-                    out=grouped_w[:],
-                    in0=raw_weights[layer][:].rearrange("p j (c m) -> p m c j", m=PACK),
-                    scalar1=sign,
-                    scalar2=0.0,
-                    op0=ALU.mult,
-                    op1=ALU.add,
+                    out=select[:, g, :], in0=wrow[:], scalar1=member[:, g : g + 1], scalar2=0.0, op0=ALU.mult, op1=ALU.add
                 )
-                nc.vector.quantize_mx(
-                    out=weight_codes[layer][:].bitcast(FP8X4),
-                    scales=weight_scales[layer][:],
-                    in_=grouped_w[:].rearrange("p m c j -> p (m c j)"),
+
+        def prepare_features():
+            raw = keep.tile([P, SPREADS, PACK, GROUPS, ROWS], BF16, name="raw_features")
+            nc.gpsimd.memset(raw[:], 1.0)
+            chosen = keep.tile([P, SPREADS, GROUPS], BF16, name="chosen")
+            nc.vector.memset(chosen[:, 3, ATOMS:GROUPS], 0.0)
+            for s in range(3):
+                nc.vector.tensor_copy(
+                    out=chosen[:, s, :].rearrange("p (j n) -> p j n", n=2),
+                    in_=d_raw[:, 2 * s + 2 : 2 * s + 4, :].rearrange("p n j -> p j n"),
                 )
+            nc.vector.tensor_copy(out=chosen[:, 3, 0:ATOMS], in_=d_raw[:, 8, :])
+            z = keep.tile([P, PACK, SPREADS * GROUPS], F32, name="z")
+            for t in range(PACK):
                 nc.vector.tensor_scalar(
-                    out=minus_bias[layer][:], in0=raw_biases[layer][:], scalar1=-1.0, scalar2=None, op0=ALU.mult,
-                )
-                nc.vector.tensor_scalar(
-                    out=guard_bias[layer][:], in0=raw_biases[layer][:], scalar1=-1.0, scalar2=LN2,
+                    out=z[:, t, :], in0=chosen[:].rearrange("p s g -> p (s g)"), scalar1=INV_STEP, scalar2=-float(t),
                     op0=ALU.mult, op1=ALU.add,
                 )
-            for a in range(2, BASIS_STEPS + 2):
-                basis_round(a)
+            z2 = keep.tile([P, PACK, SPREADS * GROUPS], F32, name="z2")
+            nc.vector.tensor_tensor(out=z2[:], in0=z[:], in1=z[:], op=ALU.mult)
+            for t in range(PACK):
+                nc.vector.memset(raw[:, :, t, :, 5], float(t))
+                for f in (3, 4):
+                    nc.vector.tensor_copy(out=raw[:, :, t, :, f], in_=chosen[:])
+            for f in range(3):
+                piece = raw[:, :, :, :, f]
+                rest = z2[:].rearrange("p t (s g) -> p s t g", g=GROUPS)
+                nc.vector.tensor_copy(out=piece, in_=rest)
+                if f < 2:
+                    nc.vector.tensor_tensor(out=rest, in0=rest, in1=piece, op=ALU.subtract)
+            return raw
 
-        with tc.tile_pool(name="layers", bufs=2, reuse_waits="tile") as work:
-            x_all = work.tile([P, OUT_TILES, FEATURES], BF16, name="x_all", bufs=1)
-            nc.sync.dma_start(out=x_all[:], in_=x_rows.rearrange("(n p) f -> p n f", p=P))
-            minus_sum = work.tile([P, PACK, ATOM_ROWS], F32, name="minus_sum", bufs=1)
-
-            def multiply(layer, c, m, bank):
-                feats = slice(m * P, (m + 1) * P)
-                cols = slice(c * CHUNK, (c + 1) * CHUNK)
-                nc.tensor.matmul_mx(
-                    out=bank[:],
-                    lhsT=weight_codes[layer][:, feats].bitcast(FP8X4),
-                    lhsT_scale=weight_scales[layer][:, feats],
-                    rhs=moving_codes[:, cols].bitcast(FP8X4),
-                    rhs_scale=moving_scales[:, cols],
-                    start=True,
-                    stop=True,
-                )
-
-            def products_for_scalar(layer, c):
-                banks = []
-                for m in range(PACK):
-                    bank = psum.tile([P, CHUNK], F32, name="bank_s", tag="for_scalar")
-                    multiply(layer, c, m, bank)
-                    banks.append(bank)
-                return banks
-
-            def sigmoid_chunk(layer, banks):
-                soft = work.tile([P, PACK, CHUNK], F32, name="soft", bufs=2 * BATCH + 2)
-                for m in range(PACK):
-                    nc.scalar.activation(
-                        out=soft[:, m, :], in_=banks[m][:], func=ACT.Sigmoid, bias=minus_bias[layer][:, m : m + 1],
-                    )
-                return soft
-
-            def log_chunk(soft):
-                nc.scalar.activation(out=soft[:], in_=soft[:], func=ACT.Ln, scale=2.0, bias=tiny[:])
-
-            def guard_chunk(layer, c, soft, result):
-                for m in range(PACK):
-                    bank = psum.tile([P, CHUNK], F32, name="bank_v", tag="for_vector")
-                    multiply(layer, c, m, bank)
-                    nc.vector.scalar_tensor_tensor(
-                        out=result[:, m, :], in0=bank[:], scalar=guard_bias[layer][:, m : m + 1], in1=soft[:, m, :],
-                        op0=ALU.add, op1=ALU.min,
-                    )
-
-            def regroup_hidden(h_planes):
-                h_grouped = work.tile([P, CHUNK, PACK], BF16, name="h_grouped", bufs=3, align_bytes=64)
+        def spread_features(raw):
+            for s in range(SPREADS):
+                turned = psum.tile([P, PACK, P], BF16, name="turned_f", tag="for_vector")
+                for t in range(PACK):
+                    nc.tensor.transpose(turned[:, t, :], raw[:, s, t, :, :].rearrange("p g r -> p (g r)"), identity_b[:])
                 nc.vector.tensor_copy(
-                    out=h_grouped[:].rearrange("p (c i) t -> p c t i", i=4),
-                    in_=h_planes[:].rearrange("p t (c i) -> p c t i", i=4),
-                )
-                return h_grouped
-
-            def quantise_hidden(c, h_grouped):
-                cols = slice(c * CHUNK, (c + 1) * CHUNK)
-                nc.vector.quantize_mx(
-                    out=moving_codes[:, cols].bitcast(FP8X4),
-                    scales=moving_scales[:, cols],
-                    in_=h_grouped[:].rearrange("p w t -> p (w t)"),
+                    out=features[:, s, :].rearrange("p (c t) -> p c t", t=PACK), in_=turned[:].rearrange("p t c -> p c t")
                 )
 
-            def sum_neighbours(c, soft):
-                rows = slice(c * CHUNK // ATOMS, (c + 1) * CHUNK // ATOMS)
-                nc.vector.tensor_reduce(
-                    out=minus_sum[:, :, rows],
-                    in_=soft[:].rearrange("p m (a j) -> p m a j", j=ATOMS),
-                    axis=mybir.AxisListType.X,
-                    op=ALU.add,
-                )
+        def multiply(layer, c, m, bank):
+            feats = slice(m * P, (m + 1) * P)
+            cols = chunk_cols(c)
+            nc.tensor.matmul_mx(
+                out=bank[:],
+                lhsT=weight_codes[layer][:, feats].bitcast(FP8X4),
+                lhsT_scale=weight_scales[layer][:, feats],
+                rhs=moving_codes[:, cols].bitcast(FP8X4),
+                rhs_scale=moving_scales[:, cols],
+                start=True,
+                stop=True,
+            )
 
-            def store_out_tile(n):
-                rows = slice(n * P, (n + 1) * P)
-                turned = psum.tile([P, PACK, P], F32, name="turned", tag="for_vector")
-                for m in range(PACK):
-                    nc.tensor.transpose(turned[:, m, :], minus_sum[:, m, rows], identity[:])
-                product = work.tile([P, FEATURES], F32, name="product")
+        items = []
+        state = {"next": 0, "credit": 0.0}
+        trailing = []
+        turns = []
+        state["turn"] = 0
+
+        def run_turn():
+            if state["turn"] < len(turns):
+                turns[state["turn"]]()
+                state["turn"] += 1
+                return True
+            return False
+
+        def run_item():
+            if state["next"] >= len(items):
+                return False
+            behind = list(trailing)
+            trailing.clear()
+            items[state["next"]][2]()
+            state["next"] += 1
+            for f in behind:
+                f()
+            run_turn()
+            return True
+
+        def run_items(credit):
+            state["credit"] += credit
+            while state["credit"] >= 1.0:
+                state["credit"] -= 1.0
+                if not run_item():
+                    run_turn()
+
+        def finish(kind, c):
+            while any(k == kind and d == c for k, d, f in items[state["next"] :]):
+                run_item()
+            for f in list(trailing):
+                f()
+            trailing.clear()
+
+        softs = {}
+        h_planes = {}
+
+        def guard_item(c, m):
+            if m == 0:
+                h_planes[c] = work.tile([P, PACK, CHUNK], BF16, name="h_planes", tag="planes", bufs=2)
+            bank = psum.tile([P, CHUNK], F32, name="bank_v", tag="for_vector")
+            multiply(HIDDEN, c, m, bank)
+            nc.vector.scalar_tensor_tensor(
+                out=h_planes[c][:, m, :], in0=bank[:], scalar=guard_bias[:, m : m + 1], in1=softs[c][:, m, :],
+                op0=ALU.add, op1=ALU.min,
+            )
+            if m == PACK - 1:
+                grouped = regroup(h_planes[c])
+                trailing.append(lambda: quantise_columns(chunk_cols(c), grouped))
+
+        sums = {}
+        products = {}
+
+        def filter_item(c, m):
+            u, k = chunk_unit[c]
+            if k == 0 and m == 0:
+                sums[u] = work.tile([P, PACK, CHUNK], F32, name="sums", bufs=3)
+                products[u] = work.tile([P, PACK, CHUNK], F32, name="products", bufs=3)
+            bank = psum.tile([P, CHUNK], F32, name="bank_v", tag="for_vector")
+            multiply(FILTER, c, m, bank)
+            if k == 0:
+                nc.vector.tensor_scalar(
+                    out=sums[u][:, m, :], in0=bank[:], scalar1=limit[:, m : m + 1],
+                    scalar2=offset[UNITS[u][1]][:, m : m + 1], op0=ALU.min, op1=ALU.add,
+                )
+            else:
                 nc.vector.scalar_tensor_tensor(
-                    out=product[:].rearrange("p (c m) -> p c m", m=PACK),
-                    in0=turned[:].rearrange("p m c -> p c m"),
-                    scalar=-1.0,
-                    in1=x_all[:, n, :].rearrange("p (c m) -> p c m", m=PACK),
-                    op0=ALU.mult,
-                    op1=ALU.mult,
+                    out=sums[u][:, m, :], in0=bank[:], scalar=limit[:, m : m + 1], in1=sums[u][:, m, :],
+                    op0=ALU.min, op1=ALU.add,
                 )
-                nc.sync.dma_start(out=out_rows[rows, :], in_=product[:])
+            if m == PACK - 1:
+                if k == 0:
+                    nc.gpsimd.tensor_scalar(
+                        out=products[u][:], in0=softs[c][:], scalar1=FLOOR, scalar2=1.0, op0=ALU.max, op1=ALU.mult
+                    )
+                else:
+                    nc.vector.scalar_tensor_tensor(
+                        out=products[u][:], in0=softs[c][:], scalar=FLOOR, in1=products[u][:], op0=ALU.max, op1=ALU.mult
+                    )
 
-            def chunks_of_batch(b):
-                return range(b * BATCH, min((b + 1) * BATCH, CHUNKS))
+        def late_item(c, m):
+            bank = psum.tile([P, CHUNK], F32, name="bank_v", tag="for_vector")
+            multiply(FILTER, c, m, bank)
+            nc.vector.scalar_tensor_tensor(
+                out=softs[c][:, m, :], in0=bank[:], scalar=guard_bias2[:, m : m + 1], in1=softs[c][:, m, :],
+                op0=ALU.add, op1=ALU.min,
+            )
 
-            guarded_hidden = []
-            guarded_filter = []
-            early_banks = products_for_scalar(HIDDEN, 0)
-            for r in range(BATCHES + 2):
-                for c, h_planes in guarded_hidden:
-                    quantise_hidden(c, regroup_hidden(h_planes))
-                for c, soft in guarded_filter:
-                    sum_neighbours(c, soft)
-                units = []
-                if r < BATCHES:
-                    units.extend([(HIDDEN, c) for c in chunks_of_batch(r)])
-                if 1 <= r <= BATCHES:
-                    units.extend([(FILTER, c) for c in chunks_of_batch(r - 1)])
-                softs = []
-                for layer, c in units:
-                    banks = early_banks if early_banks is not None else products_for_scalar(layer, c)
-                    early_banks = None
-                    softs.append(sigmoid_chunk(layer, banks))
-                for c, soft in guarded_filter:
-                    if (c + 1) % CHUNKS_PER_OUT_TILE == 0:
-                        store_out_tile(c // CHUNKS_PER_OUT_TILE)
-                if r + 1 < BATCHES:
-                    early_banks = products_for_scalar(HIDDEN, (r + 1) * BATCH)
-                guarded_hidden = []
-                guarded_filter = []
-                for (layer, c), soft in zip(units, softs):
-                    log_chunk(soft)
-                    if layer == HIDDEN:
-                        h_planes = work.tile([P, PACK, CHUNK], BF16, name="h_planes", bufs=BATCH + 1)
-                        guard_chunk(HIDDEN, c, soft, h_planes)
-                        guarded_hidden.append((c, h_planes))
-                    else:
-                        guard_chunk(FILTER, c, soft, soft)
-                        guarded_filter.append((c, soft))
+        def push_output(u, w):
+            first, width = UNITS[u]
+            n = first + w
+            slots = BLOCKS // width
+            held = {}
+
+            def turn(m):
+                if m == 0:
+                    held["bank"] = psum.tile([P, PACK, P], F32, name="turned", tag="for_vector")
+                if u in LATE:
+                    tiles = [softs[c] for c in range(CHUNKS) if chunk_unit[c][0] == u]
+                else:
+                    tiles = [sums[u], products[u]]
+                terms = [tile[:, m, (s * width + w) * P : (s * width + w + 1) * P] for tile in tiles for s in range(slots)]
+                for i, term in enumerate(terms):
+                    nc.tensor.matmul(
+                        held["bank"][:, m, :], term, identity[:],
+                        start=(i == 0), stop=(i == len(terms) - 1), is_transpose=True,
+                    )
+                if m == PACK - 1:
+                    result = work.tile([P, FEATURES], F32, name="result")
+                    nc.vector.scalar_tensor_tensor(
+                        out=result[:].rearrange("p (c m) -> p c m", m=PACK),
+                        in0=held["bank"][:].rearrange("p m c -> p c m"),
+                        scalar=-1.0,
+                        in1=x_all[:, n, :].rearrange("p (c m) -> p c m", m=PACK),
+                        op0=ALU.mult,
+                        op1=ALU.mult,
+                    )
+                    nc.sync.dma_start(out=out_rows[:, n, :], in_=result[:])
+
+            for m in range(PACK):
+                turns.append(lambda m=m: turn(m))
+
+        def sigmoid_ops(layer, c):
+            held = {}
+
+            def product(m):
+                if layer == FILTER and m == 0:
+                    finish("hidden", c)
+                bank = psum.tile([P, CHUNK], F32, name="bank_s", tag="for_scalar")
+                multiply(layer, c, m, bank)
+                held[m] = bank
+
+            def act(m):
+                if m == 0:
+                    softs[c] = work.tile([P, PACK, CHUNK], F32, name="soft", bufs=SOFTS)
+                nc.scalar.activation(
+                    out=softs[c][:, m, :], in_=held[m][:], func=ACT.Sigmoid, bias=minus_bias[layer][:, m : m + 1]
+                )
+                if layer == FILTER and m == PACK - 1 and chunk_unit[c][0] not in LATE:
+                    for q in range(PACK):
+                        items.append(("filter", c, lambda q=q: filter_item(c, q)))
+
+            return [(lambda m=m: product(m), lambda m=m: act(m), 0.5, lambda: layer == HIDDEN or c in logged) for m in range(PACK)]
+
+        logged = []
+
+        def plane_ops(c):
+            def product():
+                square_chunk(c)
+
+            def squares_act():
+                square_acts(c)
+
+            def act():
+                exp_chunk(c)
+                grouped = regroup(planes[c])
+                quantise_columns(chunk_cols(c), grouped)
+
+            return [(product, squares_act, 0.5, lambda: True), (None, act, 1.5, None)]
+
+        def log_ops(c):
+            def act():
+                nc.scalar.activation(out=softs[c][:], in_=softs[c][:], func=ACT.Ln, scale=2.0, bias=tiny[:])
+                logged.append(c)
+                for m in range(PACK):
+                    items.append(("hidden", c, lambda m=m: guard_item(c, m)))
+
+            return [(None, act, 2.0, None)]
+
+
+        def exp_ops(c):
+            held = {}
+
+            def product(i):
+                number = (c - PLANE_CHUNKS) * BLOCKS + i
+                bank = psum.tile([P, CHUNK], F32, name="bank_x", tag="for_scalar")
+                nc.tensor.matmul(
+                    bank[:], select[:, number % GROUPS, :], features[:, number // GROUPS, :], start=True, stop=True
+                )
+                held[i] = bank
+
+            def act(i):
+                if i == 0:
+                    held["grouped"] = work.tile([P, CHUNK, PACK], BF16, name="grouped", bufs=4, align_bytes=64)
+                nc.scalar.activation(
+                    out=held["grouped"][:, i * BLOCK : (i + 1) * BLOCK, :].rearrange("p c t -> p (c t)"),
+                    in_=held[i][:], func=ACT.Exp, scale=-WIDTH,
+                )
+                if i == BLOCKS - 1:
+                    quantise_columns(chunk_cols(c), held["grouped"])
+
+            return [(lambda i=i: product(i), lambda i=i: act(i), 0.5, lambda: True) for i in range(BLOCKS)]
+
+        later = []
+
+        def late_log_ops(c):
+            def act():
+                nc.scalar.activation(out=softs[c][:], in_=softs[c][:], func=ACT.Ln, scale=2.0, bias=tiny[:])
+                for m in range(PACK):
+                    items.append(("late", c, lambda m=m: late_item(c, m)))
+
+            return [(None, act, 2.0, None)]
+
+        def late_output_ops(u):
+            def act():
+                for c in range(CHUNKS):
+                    if chunk_unit[c][0] == u:
+                        finish("late", c)
+                for w in range(UNITS[u][1]):
+                    push_output(u, w)
+
+            return [(None, act, 0.0, None)]
+
+        def product_log_ops(u):
+            def act():
+                for c in range(CHUNKS):
+                    if chunk_unit[c][0] == u:
+                        finish("filter", c)
+                nc.scalar.activation(out=products[u][:], in_=products[u][:], func=ACT.Ln, scale=LOG_SCALE)
+                for w in range(UNITS[u][1]):
+                    later.append(lambda w=w: push_output(u, w))
+
+            return [(None, act, 2.0, None)]
+
+        firsts = [sum(BATCHES[:r]) for r in range(len(BATCHES) + 1)]
+        HEAD = BATCHES[0]
+        for c in range(min(2, HEAD)):
+            square_chunk(c)
+            if c == 0:
+                square_acts(0)
+        wrow, member = prepare_select()
+        prepare_layer(HIDDEN)
+        for c in range(HEAD):
+            exp_chunk(c)
+            if c + 1 < HEAD:
+                square_acts(c + 1)
+            if c + 2 < HEAD:
+                square_chunk(c + 2)
+            grouped = regroup(planes[c])
+            if c > 0:
+                quantise_columns(chunk_cols(c - 1), before)
+            before = grouped
+            if c == 0:
+                prepare_layer(FILTER)
+                prepare_biases()
+                fill_select(wrow, member)
+            if c == 1:
+                raw_features = prepare_features()
+        quantise_columns(chunk_cols(HEAD - 1), before)
+
+        ops = []
+        finished_units = []
+        late_units = []
+        for r in range(len(BATCHES) + 1):
+            new = list(range(firsts[r], firsts[r + 1])) if r < len(BATCHES) else []
+            old = list(range(firsts[r - 1], firsts[r])) if r >= 1 else []
+            if r >= 1:
+                for c in new:
+                    ops.extend(exp_ops(c) if c >= PLANE_CHUNKS else plane_ops(c))
+            for i in range(max(len(new), len(old))):
+                if i < len(old):
+                    ops.extend(sigmoid_ops(FILTER, old[i]))
+                if i < len(new):
+                    ops.extend(sigmoid_ops(HIDDEN, new[i]))
+            for c in new:
+                ops.extend(log_ops(c))
+            for c in old:
+                if chunk_unit[c][0] in LATE:
+                    ops.extend(late_log_ops(c))
+            if new:
+                for u in finished_units:
+                    ops.extend(product_log_ops(u))
+                finished_units = []
+            for c in old:
+                u, k = chunk_unit[c]
+                if u in LATE:
+                    if k == ATOMS * UNITS[u][1] // BLOCKS - 1:
+                        late_units.append(u)
+                elif k == ATOMS * UNITS[u][1] // BLOCKS - 1:
+                    finished_units.append(u)
+        for u in finished_units:
+            ops.extend(product_log_ops(u))
+        for u in late_units:
+            ops.extend(late_output_ops(u))
+
+        banked = [op for op in ops if op[0] is not None]
+        ahead = 0
+        used = 0
+        spread_done = False
+        for op in ops:
+            ready = list(later)
+            later.clear()
+            while ahead < len(banked) and ahead < used + AHEAD and banked[ahead][3]():
+                banked[ahead][0]()
+                ahead += 1
+            op[1]()
+            if op[0] is not None:
+                used += 1
+                if used == 4:
+                    spread_features(raw_features)
+            run_items(op[2])
+            for f in ready:
+                f()
+        for f in later:
+            f()
+        while run_item() or run_turn():
+            pass

@@ -371,8 +371,8 @@ def tile_cfconv_pa_t_kernel(tc, x, distances, W1, b1, W2, b2, out):
                 )
             if m == PACK - 1:
                 if k == 0:
-                    nc.gpsimd.tensor_scalar(
-                        out=products[u][:], in0=softs[c][:], scalar1=FLOOR, scalar2=1.0, op0=ALU.max, op1=ALU.mult
+                    nc.vector.tensor_scalar(
+                        out=products[u][:], in0=softs[c][:], scalar1=FLOOR, scalar2=None, op0=ALU.max
                     )
                 else:
                     nc.vector.scalar_tensor_tensor(

@@ -24,9 +24,9 @@ INV_STEP = 10.0
 WIDTH = 0.1
 LN2 = math.log(2.0)
 TINY = 2.0**-62
-CAP = 12.0
+CAP = 10.5
 FLOOR = 1.0 / (1.0 + math.exp(CAP))
-LOG_SCALE = 64.0
+LOG_SCALE = 60
 
 BLOCK = P
 CHUNK = 512
@@ -39,8 +39,17 @@ ROWS = 8
 GROUPS = P // ROWS
 SPREADS = 4
 AHEAD = 4
+LAG = 1
+WARM = 0
+WARM_TAIL = 0
+SOON = 1
+CS = 0.5
+CE = 0.5
+CL = 3.0
+SB = 4
+VB = 4
 SOFTS = 9
-LATE = [4]
+LATE_FROM = 18
 
 HIDDEN = 0
 FILTER = 1
@@ -111,7 +120,11 @@ def tile_cfconv_pa_t_kernel(tc, x, distances, W1, b1, W2, b2, out):
         guard_bias = keep.tile([P, PACK], F32, name="guard_bias")
         guard_bias2 = keep.tile([P, PACK], F32, name="guard_bias2")
         limit = keep.tile([P, PACK], F32, name="limit")
-        offset = {1: keep.tile([P, PACK], F32, name="offset1"), 2: keep.tile([P, PACK], F32, name="offset2")}
+        capped = [[c for c in range(CHUNKS) if chunk_unit[c][0] == u and c < LATE_FROM] for u in range(len(UNITS))]
+        guarded = [[c for c in range(CHUNKS) if chunk_unit[c][0] == u and c >= LATE_FROM] for u in range(len(UNITS))]
+        offset = {}
+        for steps in sorted(set(len(chunks) for chunks in capped if chunks)):
+            offset[steps] = keep.tile([P, PACK], F32, name="offset%d" % steps)
 
         def quantise_columns(cols, grouped):
             nc.vector.quantize_mx(
@@ -126,14 +139,12 @@ def tile_cfconv_pa_t_kernel(tc, x, distances, W1, b1, W2, b2, out):
         def prepare_layer(layer):
             sign = -1.0 if layer == HIDDEN else 1.0
             grouped_w = work.tile([P, PACK, P, PACK], BF16, name="grouped_w", tag="grouped", bufs=4, align_bytes=64)
-            nc.gpsimd.tensor_scalar(
-                out=grouped_w[:],
-                in0=raw_weights[layer][:].rearrange("p j (c m) -> p m c j", m=PACK),
-                scalar1=sign,
-                scalar2=0.0,
-                op0=ALU.mult,
-                op1=ALU.add,
-            )
+            for m in range(PACK):
+                nc.vector.tensor_scalar(
+                    out=grouped_w[:, m, :, :],
+                    in0=raw_weights[layer][:].rearrange("p j (c m) -> p m c j", m=PACK)[:, m, :, :],
+                    scalar1=sign, scalar2=None, op0=ALU.mult,
+                )
             nc.vector.quantize_mx(
                 out=weight_codes[layer][:].bitcast(FP8X4),
                 scales=weight_scales[layer][:],
@@ -153,11 +164,10 @@ def tile_cfconv_pa_t_kernel(tc, x, distances, W1, b1, W2, b2, out):
             nc.vector.tensor_scalar(
                 out=limit[:], in0=raw_biases[FILTER][:], scalar1=-CAP, scalar2=None, op0=ALU.add
             )
-            for width in (1, 2):
-                steps = ATOMS * width // BLOCKS
+            for steps in sorted(offset):
                 nc.vector.tensor_scalar(
-                    out=offset[width][:], in0=raw_biases[FILTER][:], scalar1=-float(steps),
-                    scalar2=steps * (CAP + LN2) - math.log(LOG_SCALE), op0=ALU.mult, op1=ALU.add,
+                    out=offset[steps][:], in0=raw_biases[FILTER][:], scalar1=-float(steps),
+                    scalar2=steps * (CAP + LN2) - steps * LOG_SCALE * LN2 / ATOMS, op0=ALU.mult, op1=ALU.add,
                 )
 
         squares = {}
@@ -165,7 +175,7 @@ def tile_cfconv_pa_t_kernel(tc, x, distances, W1, b1, W2, b2, out):
         planes = {}
 
         def square_chunk(c):
-            spread = psum.tile([P, CHUNK], BF16, name="spread", tag="for_scalar")
+            spread = psum.tile([P, CHUNK], BF16, name="spread", tag="for_scalar", bufs=SB)
             for i, (n, j) in enumerate(chunk_blocks[c]):
                 nc.tensor.transpose(
                     spread[:, i * BLOCK : (i + 1) * BLOCK],
@@ -210,36 +220,27 @@ def tile_cfconv_pa_t_kernel(tc, x, distances, W1, b1, W2, b2, out):
         select = keep.tile([P, GROUPS, P], BF16, name="select")
         features = keep.tile([P, SPREADS, CHUNK], BF16, name="features")
 
-        def prepare_select():
-            wcol = keep.tile([P, P], BF16, name="wcol")
+        MID = P - ROWS
+        window = keep.tile([P, 2 * P - ROWS], BF16, name="window")
+        nc.gpsimd.memset(window[:], 0.0)
+
+        def prepare_window():
             w32 = keep.tile([P, 2], F32, name="w32")
-            nc.vector.memset(wcol[:, 0:3], 1.0)
+            nc.vector.memset(window[:, MID : MID + 3], 1.0)
             nc.vector.tensor_scalar(out=w32[:, 0:1], in0=centre[:, 0:1], scalar1=-20.0, scalar2=None, op0=ALU.mult)
             nc.vector.tensor_tensor(out=w32[:, 1:2], in0=centre[:, 0:1], in1=centre[:, 0:1], op=ALU.mult)
-            nc.vector.tensor_copy(out=wcol[:, 3:4], in_=w32[:, 0:1])
-            nc.vector.tensor_copy(out=wcol[:, 6:7], in_=w32[:, 1:2])
-            nc.vector.tensor_scalar(out=wcol[:, 5:6], in0=centre[:, 0:1], scalar1=2.0, scalar2=None, op0=ALU.mult)
-            nc.vector.tensor_tensor(out=wcol[:, 4:5], in0=w32[:, 0:1], in1=wcol[:, 3:4], op=ALU.subtract)
-            nc.vector.tensor_tensor(out=wcol[:, 7:8], in0=w32[:, 1:2], in1=wcol[:, 6:7], op=ALU.subtract)
-            have = ROWS
-            while have < P:
-                nc.vector.tensor_copy(out=wcol[:, have : 2 * have], in_=wcol[:, 0:have])
-                have *= 2
-            member = keep.tile([P, GROUPS], F32, name="member")
-            nc.vector.tensor_reduce(
-                out=member[:], in_=identity[:].rearrange("p (g r) -> p g r", r=ROWS), axis=mybir.AxisListType.X, op=ALU.add
+            nc.vector.tensor_scalar(out=window[:, MID + 5 : MID + 6], in0=centre[:, 0:1], scalar1=2.0, scalar2=None, op0=ALU.mult)
+            nc.vector.tensor_copy(out=window[:, MID + 3 : MID + 7 : 3], in_=w32[:])
+            nc.vector.tensor_tensor(
+                out=window[:, MID + 4 : MID + 8 : 3], in0=w32[:], in1=window[:, MID + 3 : MID + 7 : 3], op=ALU.subtract
             )
-            turned = psum.tile([P, P], BF16, name="turned_w", tag="for_vector")
-            nc.tensor.transpose(turned[:], wcol[:], identity_b[:])
-            wrow = keep.tile([P, P], BF16, name="wrow")
-            nc.vector.tensor_copy(out=wrow[:], in_=turned[:])
-            return wrow, member
 
-        def fill_select(wrow, member):
-            for g in range(GROUPS):
-                nc.gpsimd.tensor_scalar(
-                    out=select[:, g, :], in0=wrow[:], scalar1=member[:, g : g + 1], scalar2=0.0, op0=ALU.mult, op1=ALU.add
-                )
+        def fill_select(quarter):
+            turned = psum.tile([P, PACK, P], BF16, name="turned_w", tag="for_vector", bufs=VB)
+            for i in range(PACK):
+                g = quarter * PACK + i
+                nc.tensor.transpose(turned[:, i, :], window[:, MID - ROWS * g : MID - ROWS * g + P], identity_b[:])
+            nc.vector.tensor_copy(out=select[:, quarter * PACK : (quarter + 1) * PACK, :], in_=turned[:])
 
         def prepare_features():
             raw = keep.tile([P, SPREADS, PACK, GROUPS, ROWS], BF16, name="raw_features")
@@ -274,7 +275,7 @@ def tile_cfconv_pa_t_kernel(tc, x, distances, W1, b1, W2, b2, out):
 
         def spread_features(raw):
             for s in range(SPREADS):
-                turned = psum.tile([P, PACK, P], BF16, name="turned_f", tag="for_vector")
+                turned = psum.tile([P, PACK, P], BF16, name="turned_f", tag="for_vector", bufs=VB)
                 for t in range(PACK):
                     nc.tensor.transpose(turned[:, t, :], raw[:, s, t, :, :].rearrange("p g r -> p (g r)"), identity_b[:])
                 nc.vector.tensor_copy(
@@ -296,9 +297,10 @@ def tile_cfconv_pa_t_kernel(tc, x, distances, W1, b1, W2, b2, out):
 
         items = []
         state = {"next": 0, "credit": 0.0}
-        trailing = []
+        waiting = []
         turns = []
         state["turn"] = 0
+        state["quiet"] = False
 
         def run_turn():
             if state["turn"] < len(turns):
@@ -307,15 +309,19 @@ def tile_cfconv_pa_t_kernel(tc, x, distances, W1, b1, W2, b2, out):
                 return True
             return False
 
+        def run_waiting():
+            for entry in list(waiting):
+                entry[0] -= 1
+                if entry[0] == 0:
+                    waiting.remove(entry)
+                    entry[1]()
+
         def run_item():
             if state["next"] >= len(items):
                 return False
-            behind = list(trailing)
-            trailing.clear()
-            items[state["next"]][2]()
             state["next"] += 1
-            for f in behind:
-                f()
+            items[state["next"] - 1][2]()
+            run_waiting()
             run_turn()
             return True
 
@@ -324,14 +330,14 @@ def tile_cfconv_pa_t_kernel(tc, x, distances, W1, b1, W2, b2, out):
             while state["credit"] >= 1.0:
                 state["credit"] -= 1.0
                 if not run_item():
+                    run_waiting()
                     run_turn()
 
         def finish(kind, c):
             while any(k == kind and d == c for k, d, f in items[state["next"] :]):
                 run_item()
-            for f in list(trailing):
-                f()
-            trailing.clear()
+            while waiting:
+                run_waiting()
 
         softs = {}
         h_planes = {}
@@ -339,30 +345,43 @@ def tile_cfconv_pa_t_kernel(tc, x, distances, W1, b1, W2, b2, out):
         def guard_item(c, m):
             if m == 0:
                 h_planes[c] = work.tile([P, PACK, CHUNK], BF16, name="h_planes", tag="planes", bufs=2)
-            bank = psum.tile([P, CHUNK], F32, name="bank_v", tag="for_vector")
+            bank = psum.tile([P, CHUNK], F32, name="bank_v", tag="for_vector", bufs=VB)
             multiply(HIDDEN, c, m, bank)
+            if WARM and state["quiet"]:
+                multiply(HIDDEN, c, m, bank)
             nc.vector.scalar_tensor_tensor(
                 out=h_planes[c][:, m, :], in0=bank[:], scalar=guard_bias[:, m : m + 1], in1=softs[c][:, m, :],
                 op0=ALU.add, op1=ALU.min,
             )
             if m == PACK - 1:
-                grouped = regroup(h_planes[c])
-                trailing.append(lambda: quantise_columns(chunk_cols(c), grouped))
+                def gather():
+                    grouped = regroup(h_planes[c])
+                    waiting.append([LAG, lambda: quantise_columns(chunk_cols(c), grouped)])
+
+                waiting.append([LAG + 1, gather])
 
         sums = {}
         products = {}
+
+        def merge(u, columns):
+            half = columns // 2
+            nc.vector.tensor_tensor(
+                out=products[u][:, :, 0:half], in0=products[u][:, :, 0:half], in1=products[u][:, :, half:columns], op=ALU.mult
+            )
+            if half > UNITS[u][1] * P:
+                waiting.append([1, lambda: merge(u, half)])
 
         def filter_item(c, m):
             u, k = chunk_unit[c]
             if k == 0 and m == 0:
                 sums[u] = work.tile([P, PACK, CHUNK], F32, name="sums", bufs=3)
                 products[u] = work.tile([P, PACK, CHUNK], F32, name="products", bufs=3)
-            bank = psum.tile([P, CHUNK], F32, name="bank_v", tag="for_vector")
+            bank = psum.tile([P, CHUNK], F32, name="bank_v", tag="for_vector", bufs=VB)
             multiply(FILTER, c, m, bank)
             if k == 0:
                 nc.vector.tensor_scalar(
                     out=sums[u][:, m, :], in0=bank[:], scalar1=limit[:, m : m + 1],
-                    scalar2=offset[UNITS[u][1]][:, m : m + 1], op0=ALU.min, op1=ALU.add,
+                    scalar2=offset[len(capped[u])][:, m : m + 1], op0=ALU.min, op1=ALU.add,
                 )
             else:
                 nc.vector.scalar_tensor_tensor(
@@ -372,16 +391,21 @@ def tile_cfconv_pa_t_kernel(tc, x, distances, W1, b1, W2, b2, out):
             if m == PACK - 1:
                 if k == 0:
                     nc.vector.tensor_scalar(
-                        out=products[u][:], in0=softs[c][:], scalar1=FLOOR, scalar2=None, op0=ALU.max
+                        out=products[u][:], in0=softs[c][:], scalar1=FLOOR,
+                        scalar2=2.0 ** (LOG_SCALE * len(capped[u]) // ATOMS), op0=ALU.max, op1=ALU.mult,
                     )
                 else:
                     nc.vector.scalar_tensor_tensor(
                         out=products[u][:], in0=softs[c][:], scalar=FLOOR, in1=products[u][:], op0=ALU.max, op1=ALU.mult
                     )
+                if c == capped[u][-1]:
+                    waiting.append([1, lambda: merge(u, CHUNK)])
 
         def late_item(c, m):
-            bank = psum.tile([P, CHUNK], F32, name="bank_v", tag="for_vector")
+            bank = psum.tile([P, CHUNK], F32, name="bank_v", tag="for_vector", bufs=VB)
             multiply(FILTER, c, m, bank)
+            if WARM_TAIL:
+                multiply(FILTER, c, m, bank)
             nc.vector.scalar_tensor_tensor(
                 out=softs[c][:, m, :], in0=bank[:], scalar=guard_bias2[:, m : m + 1], in1=softs[c][:, m, :],
                 op0=ALU.add, op1=ALU.min,
@@ -395,12 +419,12 @@ def tile_cfconv_pa_t_kernel(tc, x, distances, W1, b1, W2, b2, out):
 
             def turn(m):
                 if m == 0:
-                    held["bank"] = psum.tile([P, PACK, P], F32, name="turned", tag="for_vector")
-                if u in LATE:
-                    tiles = [softs[c] for c in range(CHUNKS) if chunk_unit[c][0] == u]
-                else:
-                    tiles = [sums[u], products[u]]
+                    held["bank"] = psum.tile([P, PACK, P], F32, name="turned", tag="for_vector", bufs=VB)
+                tiles = [sums[u]] if capped[u] else []
+                tiles.extend([softs[c] for c in guarded[u]])
                 terms = [tile[:, m, (s * width + w) * P : (s * width + w + 1) * P] for tile in tiles for s in range(slots)]
+                if capped[u]:
+                    terms.append(products[u][:, m, w * P : (w + 1) * P])
                 for i, term in enumerate(terms):
                     nc.tensor.matmul(
                         held["bank"][:, m, :], term, identity[:],
@@ -418,8 +442,7 @@ def tile_cfconv_pa_t_kernel(tc, x, distances, W1, b1, W2, b2, out):
                     )
                     nc.sync.dma_start(out=out_rows[:, n, :], in_=result[:])
 
-            for m in range(PACK):
-                turns.append(lambda m=m: turn(m))
+            return [lambda m=m: turn(m) for m in range(PACK)]
 
         def sigmoid_ops(layer, c):
             held = {}
@@ -427,7 +450,7 @@ def tile_cfconv_pa_t_kernel(tc, x, distances, W1, b1, W2, b2, out):
             def product(m):
                 if layer == FILTER and m == 0:
                     finish("hidden", c)
-                bank = psum.tile([P, CHUNK], F32, name="bank_s", tag="for_scalar")
+                bank = psum.tile([P, CHUNK], F32, name="bank_s", tag="for_scalar", bufs=SB)
                 multiply(layer, c, m, bank)
                 held[m] = bank
 
@@ -437,11 +460,11 @@ def tile_cfconv_pa_t_kernel(tc, x, distances, W1, b1, W2, b2, out):
                 nc.scalar.activation(
                     out=softs[c][:, m, :], in_=held[m][:], func=ACT.Sigmoid, bias=minus_bias[layer][:, m : m + 1]
                 )
-                if layer == FILTER and m == PACK - 1 and chunk_unit[c][0] not in LATE:
+                if layer == FILTER and m == PACK - 1 and c < LATE_FROM:
                     for q in range(PACK):
                         items.append(("filter", c, lambda q=q: filter_item(c, q)))
 
-            return [(lambda m=m: product(m), lambda m=m: act(m), 0.5, lambda: layer == HIDDEN or c in logged) for m in range(PACK)]
+            return [(lambda m=m: product(m), lambda m=m: act(m), CS, lambda: layer == HIDDEN or c in logged) for m in range(PACK)]
 
         logged = []
 
@@ -466,7 +489,7 @@ def tile_cfconv_pa_t_kernel(tc, x, distances, W1, b1, W2, b2, out):
                 for m in range(PACK):
                     items.append(("hidden", c, lambda m=m: guard_item(c, m)))
 
-            return [(None, act, 2.0, None)]
+            return [(None, act, CL, None)]
 
 
         def exp_ops(c):
@@ -474,7 +497,7 @@ def tile_cfconv_pa_t_kernel(tc, x, distances, W1, b1, W2, b2, out):
 
             def product(i):
                 number = (c - PLANE_CHUNKS) * BLOCKS + i
-                bank = psum.tile([P, CHUNK], F32, name="bank_x", tag="for_scalar")
+                bank = psum.tile([P, CHUNK], F32, name="bank_x", tag="for_scalar", bufs=SB)
                 nc.tensor.matmul(
                     bank[:], select[:, number % GROUPS, :], features[:, number // GROUPS, :], start=True, stop=True
                 )
@@ -490,36 +513,44 @@ def tile_cfconv_pa_t_kernel(tc, x, distances, W1, b1, W2, b2, out):
                 if i == BLOCKS - 1:
                     quantise_columns(chunk_cols(c), held["grouped"])
 
-            return [(lambda i=i: product(i), lambda i=i: act(i), 0.5, lambda: True) for i in range(BLOCKS)]
+            return [(lambda i=i: product(i), lambda i=i: act(i), CE, lambda: True) for i in range(BLOCKS)]
 
         later = []
 
         def late_log_ops(c):
-            def act():
-                nc.scalar.activation(out=softs[c][:], in_=softs[c][:], func=ACT.Ln, scale=2.0, bias=tiny[:])
-                for m in range(PACK):
-                    items.append(("late", c, lambda m=m: late_item(c, m)))
+            u, k = chunk_unit[c]
+            last = c == guarded[u][-1]
+            held = {}
 
-            return [(None, act, 2.0, None)]
+            def guard_and_turn(m):
+                late_item(c, m)
+                if last and UNITS[u][1] == 1:
+                    if m == 0:
+                        held["turns"] = push_output(u, 0)
+                    turns.append(held["turns"][m])
+                elif last and m == PACK - 1:
+                    for w in range(UNITS[u][1]):
+                        turns.extend(push_output(u, w))
 
-        def late_output_ops(u):
-            def act():
-                for c in range(CHUNKS):
-                    if chunk_unit[c][0] == u:
-                        finish("late", c)
-                for w in range(UNITS[u][1]):
-                    push_output(u, w)
+            def act(m):
+                nc.scalar.activation(
+                    out=softs[c][:, m, :], in_=softs[c][:, m, :], func=ACT.Ln, scale=2.0, bias=tiny[:]
+                )
+                items.append(("late", c, lambda: guard_and_turn(m)))
 
-            return [(None, act, 0.0, None)]
+            return [(None, lambda m=m: act(m), 0.5, None) for m in range(PACK)]
 
         def product_log_ops(u):
             def act():
-                for c in range(CHUNKS):
-                    if chunk_unit[c][0] == u:
-                        finish("filter", c)
-                nc.scalar.activation(out=products[u][:], in_=products[u][:], func=ACT.Ln, scale=LOG_SCALE)
-                for w in range(UNITS[u][1]):
-                    later.append(lambda w=w: push_output(u, w))
+                for c in capped[u]:
+                    finish("filter", c)
+                while waiting:
+                    run_waiting()
+                merged = products[u][:, :, 0 : UNITS[u][1] * P]
+                nc.scalar.activation(out=merged, in_=merged, func=ACT.Ln)
+                if not guarded[u]:
+                    for w in range(UNITS[u][1]):
+                        later.append(lambda w=w: turns.extend(push_output(u, w)))
 
             return [(None, act, 2.0, None)]
 
@@ -529,8 +560,6 @@ def tile_cfconv_pa_t_kernel(tc, x, distances, W1, b1, W2, b2, out):
             square_chunk(c)
             if c == 0:
                 square_acts(0)
-        wrow, member = prepare_select()
-        prepare_layer(HIDDEN)
         for c in range(HEAD):
             exp_chunk(c)
             if c + 1 < HEAD:
@@ -541,17 +570,22 @@ def tile_cfconv_pa_t_kernel(tc, x, distances, W1, b1, W2, b2, out):
             if c > 0:
                 quantise_columns(chunk_cols(c - 1), before)
             before = grouped
-            if c == 0:
-                prepare_layer(FILTER)
-                prepare_biases()
-                fill_select(wrow, member)
             if c == 1:
-                raw_features = prepare_features()
+                prepare_layer(HIDDEN)
         quantise_columns(chunk_cols(HEAD - 1), before)
+        prepare_window()
+        prepare_biases()
+        raw_features = prepare_features()
+        def before_first_squares():
+            for quarter in range(GROUPS // PACK):
+                fill_select(quarter)
+            spread_features(raw_features)
+            prepare_layer(FILTER)
+
+        hooks = {PACK * HEAD: before_first_squares}
 
         ops = []
         finished_units = []
-        late_units = []
         for r in range(len(BATCHES) + 1):
             new = list(range(firsts[r], firsts[r + 1])) if r < len(BATCHES) else []
             old = list(range(firsts[r - 1], firsts[r])) if r >= 1 else []
@@ -565,40 +599,32 @@ def tile_cfconv_pa_t_kernel(tc, x, distances, W1, b1, W2, b2, out):
                     ops.extend(sigmoid_ops(HIDDEN, new[i]))
             for c in new:
                 ops.extend(log_ops(c))
-            for c in old:
-                if chunk_unit[c][0] in LATE:
-                    ops.extend(late_log_ops(c))
-            if new:
+            for u in finished_units:
+                ops.extend(product_log_ops(u))
+            finished_units = [chunk_unit[c][0] for c in old if c in [chunks[-1] for chunks in capped if chunks]]
+            if not new or SOON:
                 for u in finished_units:
                     ops.extend(product_log_ops(u))
                 finished_units = []
             for c in old:
-                u, k = chunk_unit[c]
-                if u in LATE:
-                    if k == ATOMS * UNITS[u][1] // BLOCKS - 1:
-                        late_units.append(u)
-                elif k == ATOMS * UNITS[u][1] // BLOCKS - 1:
-                    finished_units.append(u)
-        for u in finished_units:
-            ops.extend(product_log_ops(u))
-        for u in late_units:
-            ops.extend(late_output_ops(u))
+                if c >= LATE_FROM:
+                    ops.extend(late_log_ops(c))
 
         banked = [op for op in ops if op[0] is not None]
         ahead = 0
         used = 0
-        spread_done = False
         for op in ops:
             ready = list(later)
             later.clear()
             while ahead < len(banked) and ahead < used + AHEAD and banked[ahead][3]():
+                if ahead in hooks:
+                    hooks[ahead]()
                 banked[ahead][0]()
                 ahead += 1
             op[1]()
+            state["quiet"] = op[0] is None
             if op[0] is not None:
                 used += 1
-                if used == 4:
-                    spread_features(raw_features)
             run_items(op[2])
             for f in ready:
                 f()

@@ -39,17 +39,19 @@ ROWS = 8
 GROUPS = P // ROWS
 SPREADS = 4
 AHEAD = 4
+MARGIN = 1
 LAG = 1
 WARM = 0
 WARM_TAIL = 0
 SOON = 1
 CS = 0.5
-CE = 0.5
+CE = 0.4
 CL = 3.0
 SB = 4
 VB = 4
 SOFTS = 9
-LATE_FROM = 18
+SUMS = 2
+LATE_FROM = 16
 
 HIDDEN = 0
 FILTER = 1
@@ -85,8 +87,6 @@ def tile_cfconv_pa_t_kernel(tc, x, distances, W1, b1, W2, b2, out):
             raw_b = keep.tile([P, PACK], BF16, name="raw_b%d" % layer)
             nc.sync.dma_start(out=raw_b[:], in_=bias.rearrange("(c m) -> c m", m=PACK))
             raw_biases.append(raw_b)
-        x_all = keep.tile([P, TILES, FEATURES], BF16, name="x_all")
-        nc.sync.dma_start(out=x_all[:], in_=x_rows)
 
         identity_b = keep.tile([P, P], BF16, name="identity_b")
         make_identity(nc, identity_b[:])
@@ -333,9 +333,12 @@ def tile_cfconv_pa_t_kernel(tc, x, distances, W1, b1, W2, b2, out):
                     run_waiting()
                     run_turn()
 
-        def finish(kind, c):
+        def finish_items(kind, c):
             while any(k == kind and d == c for k, d, f in items[state["next"] :]):
                 run_item()
+
+        def finish(kind, c):
+            finish_items(kind, c)
             while waiting:
                 run_waiting()
 
@@ -374,8 +377,8 @@ def tile_cfconv_pa_t_kernel(tc, x, distances, W1, b1, W2, b2, out):
         def filter_item(c, m):
             u, k = chunk_unit[c]
             if k == 0 and m == 0:
-                sums[u] = work.tile([P, PACK, CHUNK], F32, name="sums", bufs=3)
-                products[u] = work.tile([P, PACK, CHUNK], F32, name="products", bufs=3)
+                sums[u] = work.tile([P, PACK, CHUNK], F32, name="sums", bufs=SUMS)
+                products[u] = work.tile([P, PACK, CHUNK], F32, name="products", bufs=SUMS)
             bank = psum.tile([P, CHUNK], F32, name="bank_v", tag="for_vector", bufs=VB)
             multiply(FILTER, c, m, bank)
             if k == 0:
@@ -416,6 +419,8 @@ def tile_cfconv_pa_t_kernel(tc, x, distances, W1, b1, W2, b2, out):
             n = first + w
             slots = BLOCKS // width
             held = {}
+            x_tile = work.tile([P, FEATURES], BF16, name="x_tile", bufs=4)
+            nc.sync.dma_start(out=x_tile[:], in_=x_rows[:, n, :])
 
             def turn(m):
                 if m == 0:
@@ -436,7 +441,7 @@ def tile_cfconv_pa_t_kernel(tc, x, distances, W1, b1, W2, b2, out):
                         out=result[:].rearrange("p (c m) -> p c m", m=PACK),
                         in0=held["bank"][:].rearrange("p m c -> p c m"),
                         scalar=-1.0,
-                        in1=x_all[:, n, :].rearrange("p (c m) -> p c m", m=PACK),
+                        in1=x_tile[:].rearrange("p (c m) -> p c m", m=PACK),
                         op0=ALU.mult,
                         op1=ALU.mult,
                     )
@@ -449,6 +454,8 @@ def tile_cfconv_pa_t_kernel(tc, x, distances, W1, b1, W2, b2, out):
 
             def product(m):
                 if layer == FILTER and m == 0:
+                    for d in range(c, min(c + MARGIN + 1, CHUNKS)):
+                        finish_items("hidden", d)
                     finish("hidden", c)
                 bank = psum.tile([P, CHUNK], F32, name="bank_s", tag="for_scalar", bufs=SB)
                 multiply(layer, c, m, bank)
@@ -524,11 +531,7 @@ def tile_cfconv_pa_t_kernel(tc, x, distances, W1, b1, W2, b2, out):
 
             def guard_and_turn(m):
                 late_item(c, m)
-                if last and UNITS[u][1] == 1:
-                    if m == 0:
-                        held["turns"] = push_output(u, 0)
-                    turns.append(held["turns"][m])
-                elif last and m == PACK - 1:
+                if last and m == PACK - 1:
                     for w in range(UNITS[u][1]):
                         turns.extend(push_output(u, w))
 
@@ -601,14 +604,14 @@ def tile_cfconv_pa_t_kernel(tc, x, distances, W1, b1, W2, b2, out):
                 ops.extend(log_ops(c))
             for u in finished_units:
                 ops.extend(product_log_ops(u))
+            for c in old:
+                if c >= LATE_FROM:
+                    ops.extend(late_log_ops(c))
             finished_units = [chunk_unit[c][0] for c in old if c in [chunks[-1] for chunks in capped if chunks]]
             if not new or SOON:
                 for u in finished_units:
                     ops.extend(product_log_ops(u))
                 finished_units = []
-            for c in old:
-                if c >= LATE_FROM:
-                    ops.extend(late_log_ops(c))
 
         banked = [op for op in ops if op[0] is not None]
         ahead = 0

@@ -24,9 +24,9 @@ INV_STEP = 10.0
 WIDTH = 0.1
 LN2 = math.log(2.0)
 TINY = 2.0**-62
-CAP = 10.5
+CAP = 10.35
 FLOOR = 1.0 / (1.0 + math.exp(CAP))
-LOG_SCALE = 60
+LOG_SCALE = 56
 
 BLOCK = P
 CHUNK = 512
@@ -51,7 +51,7 @@ SB = 4
 VB = 4
 SOFTS = 9
 SUMS = 2
-LATE_FROM = 16
+LATE = [16, 17]
 
 HIDDEN = 0
 FILTER = 1
@@ -120,8 +120,8 @@ def tile_cfconv_pa_t_kernel(tc, x, distances, W1, b1, W2, b2, out):
         guard_bias = keep.tile([P, PACK], F32, name="guard_bias")
         guard_bias2 = keep.tile([P, PACK], F32, name="guard_bias2")
         limit = keep.tile([P, PACK], F32, name="limit")
-        capped = [[c for c in range(CHUNKS) if chunk_unit[c][0] == u and c < LATE_FROM] for u in range(len(UNITS))]
-        guarded = [[c for c in range(CHUNKS) if chunk_unit[c][0] == u and c >= LATE_FROM] for u in range(len(UNITS))]
+        capped = [[c for c in range(CHUNKS) if chunk_unit[c][0] == u and c not in LATE] for u in range(len(UNITS))]
+        guarded = [[c for c in range(CHUNKS) if chunk_unit[c][0] == u and c in LATE] for u in range(len(UNITS))]
         offset = {}
         for steps in sorted(set(len(chunks) for chunks in capped if chunks)):
             offset[steps] = keep.tile([P, PACK], F32, name="offset%d" % steps)
@@ -376,12 +376,12 @@ def tile_cfconv_pa_t_kernel(tc, x, distances, W1, b1, W2, b2, out):
 
         def filter_item(c, m):
             u, k = chunk_unit[c]
-            if k == 0 and m == 0:
+            if c == capped[u][0] and m == 0:
                 sums[u] = work.tile([P, PACK, CHUNK], F32, name="sums", bufs=SUMS)
                 products[u] = work.tile([P, PACK, CHUNK], F32, name="products", bufs=SUMS)
             bank = psum.tile([P, CHUNK], F32, name="bank_v", tag="for_vector", bufs=VB)
             multiply(FILTER, c, m, bank)
-            if k == 0:
+            if c == capped[u][0]:
                 nc.vector.tensor_scalar(
                     out=sums[u][:, m, :], in0=bank[:], scalar1=limit[:, m : m + 1],
                     scalar2=offset[len(capped[u])][:, m : m + 1], op0=ALU.min, op1=ALU.add,
@@ -392,7 +392,7 @@ def tile_cfconv_pa_t_kernel(tc, x, distances, W1, b1, W2, b2, out):
                     op0=ALU.min, op1=ALU.add,
                 )
             if m == PACK - 1:
-                if k == 0:
+                if c == capped[u][0]:
                     nc.vector.tensor_scalar(
                         out=products[u][:], in0=softs[c][:], scalar1=FLOOR,
                         scalar2=2.0 ** (LOG_SCALE * len(capped[u]) // ATOMS), op0=ALU.max, op1=ALU.mult,
@@ -467,11 +467,11 @@ def tile_cfconv_pa_t_kernel(tc, x, distances, W1, b1, W2, b2, out):
                 nc.scalar.activation(
                     out=softs[c][:, m, :], in_=held[m][:], func=ACT.Sigmoid, bias=minus_bias[layer][:, m : m + 1]
                 )
-                if layer == FILTER and m == PACK - 1 and c < LATE_FROM:
+                if layer == FILTER and m == PACK - 1 and c not in LATE:
                     for q in range(PACK):
                         items.append(("filter", c, lambda q=q: filter_item(c, q)))
 
-            return [(lambda m=m: product(m), lambda m=m: act(m), CS, lambda: layer == HIDDEN or c in logged) for m in range(PACK)]
+            return [(lambda m=m: product(m), lambda m=m: act(m), CS, lambda: layer == HIDDEN or min(c + MARGIN, CHUNKS - 1) in logged or (c in logged and c + 1 in firsts)) for m in range(PACK)]
 
         logged = []
 
@@ -605,7 +605,7 @@ def tile_cfconv_pa_t_kernel(tc, x, distances, W1, b1, W2, b2, out):
             for u in finished_units:
                 ops.extend(product_log_ops(u))
             for c in old:
-                if c >= LATE_FROM:
+                if c in LATE:
                     ops.extend(late_log_ops(c))
             finished_units = [chunk_unit[c][0] for c in old if c in [chunks[-1] for chunks in capped if chunks]]
             if not new or SOON:

@@ -41,6 +41,8 @@ SPREADS = 4
 AHEAD = 4
 MARGIN = 1
 LAG = 1
+HEADSTART = 0
+PLANES = 4
 WARM = 0
 WARM_TAIL = 0
 SOON = 1
@@ -49,7 +51,7 @@ CE = 0.4
 CL = 3.0
 SB = 4
 VB = 4
-SOFTS = 9
+SOFTS = 10
 SUMS = 2
 LATE = [16, 17]
 
@@ -88,23 +90,31 @@ def tile_cfconv_pa_t_kernel(tc, x, distances, W1, b1, W2, b2, out):
             nc.sync.dma_start(out=raw_b[:], in_=bias.rearrange("(c m) -> c m", m=PACK))
             raw_biases.append(raw_b)
 
-        identity_b = keep.tile([P, P], BF16, name="identity_b")
-        make_identity(nc, identity_b[:])
         centre_int = keep.tile([P, PACK], I32, name="centre_int")
         nc.gpsimd.iota(centre_int[:], pattern=[[1, PACK]], base=0, channel_multiplier=PACK)
+        window = keep.tile([P, 2 * P - ROWS], BF16, name="window")
+        nc.gpsimd.memset(window[:], 0.0)
+        identity_b = keep.tile([P, P], BF16, name="identity_b")
+        make_identity(nc, identity_b[:])
+        whole = keep.tile([P, PACK], F32, name="whole")
+        for t in range(PACK):
+            nc.gpsimd.memset(whole[:, t : t + 1], float(t * (t - 1)))
+        tiny = keep.tile([P, 1], F32, name="tiny")
+        nc.gpsimd.memset(tiny[:], TINY)
+        raw = keep.tile([P, SPREADS, PACK, GROUPS, ROWS], BF16, name="raw_features")
+        nc.gpsimd.memset(raw[:], 1.0)
+        minus_t = keep.tile([P, PACK, 1], F32, name="minus_t")
+        for t in range(PACK):
+            nc.gpsimd.memset(raw[:, :, t, :, 5], float(t))
+            nc.gpsimd.memset(minus_t[:, t, :], -float(t))
+        chosen = keep.tile([P, SPREADS, GROUPS], BF16, name="chosen")
+        nc.gpsimd.memset(chosen[:, 3, ATOMS:GROUPS], 0.0)
         identity = keep.tile([P, P], F32, name="identity")
         make_identity(nc, identity[:])
         centre = keep.tile([P, PACK], F32, name="centre")
         nc.vector.tensor_copy(out=centre[:], in_=centre_int[:])
         minus_centre = keep.tile([P, PACK], F32, name="minus_centre")
         nc.vector.tensor_scalar(out=minus_centre[:], in0=centre[:], scalar1=-1.0, scalar2=None, op0=ALU.mult)
-        whole = keep.tile([P, PACK], F32, name="whole")
-        for t in range(PACK):
-            nc.vector.memset(whole[:, t : t + 1], float(t * (t - 1)))
-        exp_bias = keep.tile([P, PACK], F32, name="exp_bias")
-        nc.vector.tensor_scalar(out=exp_bias[:], in0=whole[:], scalar1=-WIDTH, scalar2=None, op0=ALU.mult)
-        tiny = keep.tile([P, 1], F32, name="tiny")
-        nc.vector.memset(tiny[:], TINY)
 
         moving_codes = keep.tile([P, PAIRS], U32, name="moving_codes", align_bytes=64)
         moving_scales = keep.tile([P, PAIRS], U8, name="moving_scales", align_bytes=64)
@@ -116,6 +126,7 @@ def tile_cfconv_pa_t_kernel(tc, x, distances, W1, b1, W2, b2, out):
             keep.tile([P, FEATURES], U8, name="w1_scales", align_bytes=64),
             keep.tile([P, FEATURES], U8, name="w2_scales", align_bytes=64),
         ]
+        exp_bias = keep.tile([P, PACK], F32, name="exp_bias")
         minus_bias = [keep.tile([P, PACK], F32, name="minus_b1"), keep.tile([P, PACK], F32, name="minus_b2")]
         guard_bias = keep.tile([P, PACK], F32, name="guard_bias")
         guard_bias2 = keep.tile([P, PACK], F32, name="guard_bias2")
@@ -136,7 +147,9 @@ def tile_cfconv_pa_t_kernel(tc, x, distances, W1, b1, W2, b2, out):
         def chunk_cols(c):
             return slice(c * CHUNK, (c + 1) * CHUNK)
 
-        def prepare_layer(layer):
+        grouped_weights = {}
+
+        def group_weights(layer):
             sign = -1.0 if layer == HIDDEN else 1.0
             grouped_w = work.tile([P, PACK, P, PACK], BF16, name="grouped_w", tag="grouped", bufs=4, align_bytes=64)
             for m in range(PACK):
@@ -145,27 +158,32 @@ def tile_cfconv_pa_t_kernel(tc, x, distances, W1, b1, W2, b2, out):
                     in0=raw_weights[layer][:].rearrange("p j (c m) -> p m c j", m=PACK)[:, m, :, :],
                     scalar1=sign, scalar2=None, op0=ALU.mult,
                 )
+            grouped_weights[layer] = grouped_w
+
+        def quantise_weights(layer):
             nc.vector.quantize_mx(
                 out=weight_codes[layer][:].bitcast(FP8X4),
                 scales=weight_scales[layer][:],
-                in_=grouped_w[:].rearrange("p m c j -> p (m c j)"),
-            )
-            nc.vector.tensor_scalar(
-                out=minus_bias[layer][:], in0=raw_biases[layer][:], scalar1=-1.0, scalar2=None, op0=ALU.mult
+                in_=grouped_weights[layer][:].rearrange("p m c j -> p (m c j)"),
             )
 
         def prepare_biases():
-            nc.vector.tensor_scalar(
+            nc.gpsimd.tensor_scalar(out=exp_bias[:], in0=whole[:], scalar1=-WIDTH, scalar2=0.0, op0=ALU.mult, op1=ALU.add)
+            for layer in (HIDDEN, FILTER):
+                nc.gpsimd.tensor_scalar(
+                    out=minus_bias[layer][:], in0=raw_biases[layer][:], scalar1=-1.0, scalar2=0.0, op0=ALU.mult, op1=ALU.add
+                )
+            nc.gpsimd.tensor_scalar(
                 out=guard_bias[:], in0=raw_biases[HIDDEN][:], scalar1=-1.0, scalar2=LN2, op0=ALU.mult, op1=ALU.add
             )
-            nc.vector.tensor_scalar(
+            nc.gpsimd.tensor_scalar(
                 out=guard_bias2[:], in0=raw_biases[FILTER][:], scalar1=-1.0, scalar2=LN2, op0=ALU.mult, op1=ALU.add
             )
-            nc.vector.tensor_scalar(
-                out=limit[:], in0=raw_biases[FILTER][:], scalar1=-CAP, scalar2=None, op0=ALU.add
+            nc.gpsimd.tensor_scalar(
+                out=limit[:], in0=raw_biases[FILTER][:], scalar1=1.0, scalar2=-CAP, op0=ALU.mult, op1=ALU.add
             )
             for steps in sorted(offset):
-                nc.vector.tensor_scalar(
+                nc.gpsimd.tensor_scalar(
                     out=offset[steps][:], in0=raw_biases[FILTER][:], scalar1=-float(steps),
                     scalar2=steps * (CAP + LN2) - steps * LOG_SCALE * LN2 / ATOMS, op0=ALU.mult, op1=ALU.add,
                 )
@@ -184,23 +202,35 @@ def tile_cfconv_pa_t_kernel(tc, x, distances, W1, b1, W2, b2, out):
                 )
             spreads[c] = spread
 
-        def square_acts(c):
-            spread = spreads[c]
-            sq = work.tile([P, PACK, CHUNK], F32, name="sq", tag="soft", bufs=SOFTS)
-            for t in range(2):
-                nc.scalar.activation(
-                    out=sq[:, t, :], in_=spread[:], func=ACT.Square, scale=INV_STEP, bias=minus_centre[:, t : t + 1]
-                )
+        shifted = {}
+
+        def square_base(c):
+            squares[c] = work.tile([P, PACK, CHUNK], F32, name="sq", tag="soft", bufs=SOFTS)
+            nc.scalar.activation(
+                out=squares[c][:, 0, :], in_=spreads[c][:], func=ACT.Square, scale=INV_STEP, bias=minus_centre[:, 0:1]
+            )
+
+        def shift_distance(c):
+            shifted[c] = work.tile([P, CHUNK], F32, name="shifted")
+            nc.vector.tensor_scalar(
+                out=shifted[c][:], in0=spreads[c][:], scalar1=INV_STEP, scalar2=minus_centre[:, 1:2],
+                op0=ALU.mult, op1=ALU.add,
+            )
+
+        def square_next(c):
+            nc.vector.tensor_tensor(out=squares[c][:, 1, :], in0=shifted[c][:], in1=shifted[c][:], op=ALU.mult)
+
+        def square_rest(c):
+            sq = squares[c]
             for t in range(2, PACK):
                 nc.vector.scalar_tensor_tensor(
                     out=sq[:, t, :], in0=sq[:, 1, :], scalar=t / (t - 1.0), in1=sq[:, 0, :],
                     op0=ALU.mult, op1=ALU.subtract,
                 )
-            squares[c] = sq
 
         def exp_chunk(c):
             sq = squares[c]
-            e_planes = work.tile([P, PACK, CHUNK], BF16, name="e_planes", tag="planes", bufs=2)
+            e_planes = work.tile([P, PACK, CHUNK], BF16, name="e_planes", tag="planes", bufs=PLANES)
             nc.scalar.activation(out=e_planes[:, 0:2, :], in_=sq[:, 0:2, :], func=ACT.Exp, scale=-WIDTH)
             for t in range(2, PACK):
                 nc.scalar.activation(
@@ -221,8 +251,6 @@ def tile_cfconv_pa_t_kernel(tc, x, distances, W1, b1, W2, b2, out):
         features = keep.tile([P, SPREADS, CHUNK], BF16, name="features")
 
         MID = P - ROWS
-        window = keep.tile([P, 2 * P - ROWS], BF16, name="window")
-        nc.gpsimd.memset(window[:], 0.0)
 
         def prepare_window():
             w32 = keep.tile([P, 2], F32, name="w32")
@@ -243,37 +271,32 @@ def tile_cfconv_pa_t_kernel(tc, x, distances, W1, b1, W2, b2, out):
             nc.vector.tensor_copy(out=select[:, quarter * PACK : (quarter + 1) * PACK, :], in_=turned[:])
 
         def prepare_features():
-            raw = keep.tile([P, SPREADS, PACK, GROUPS, ROWS], BF16, name="raw_features")
-            nc.gpsimd.memset(raw[:], 1.0)
-            chosen = keep.tile([P, SPREADS, GROUPS], BF16, name="chosen")
-            nc.vector.memset(chosen[:, 3, ATOMS:GROUPS], 0.0)
             for s in range(3):
                 nc.vector.tensor_copy(
                     out=chosen[:, s, :].rearrange("p (j n) -> p j n", n=2),
                     in_=d_raw[:, 2 * s + 2 : 2 * s + 4, :].rearrange("p n j -> p j n"),
                 )
             nc.vector.tensor_copy(out=chosen[:, 3, 0:ATOMS], in_=d_raw[:, 8, :])
-            z = keep.tile([P, PACK, SPREADS * GROUPS], F32, name="z")
-            for t in range(PACK):
-                nc.vector.tensor_scalar(
-                    out=z[:, t, :], in0=chosen[:].rearrange("p s g -> p (s g)"), scalar1=INV_STEP, scalar2=-float(t),
-                    op0=ALU.mult, op1=ALU.add,
-                )
-            z2 = keep.tile([P, PACK, SPREADS * GROUPS], F32, name="z2")
+            shape = [P, PACK, SPREADS * GROUPS]
+            z = keep.tile(shape, F32, name="z")
+            nc.vector.scalar_tensor_tensor(
+                out=z[:], in0=chosen[:].rearrange("p s (o g) -> p o (s g)", o=1).to_broadcast(shape), scalar=INV_STEP,
+                in1=minus_t[:].to_broadcast(shape), op0=ALU.mult, op1=ALU.add,
+            )
+            z2 = keep.tile(shape, F32, name="z2")
             nc.vector.tensor_tensor(out=z2[:], in0=z[:], in1=z[:], op=ALU.mult)
-            for t in range(PACK):
-                nc.vector.memset(raw[:, :, t, :, 5], float(t))
-                for f in (3, 4):
-                    nc.vector.tensor_copy(out=raw[:, :, t, :, f], in_=chosen[:])
+            rest = z2[:].rearrange("p t (s g) -> p s t g", g=GROUPS)
             for f in range(3):
                 piece = raw[:, :, :, :, f]
-                rest = z2[:].rearrange("p t (s g) -> p s t g", g=GROUPS)
                 nc.vector.tensor_copy(out=piece, in_=rest)
                 if f < 2:
+                    nc.vector.tensor_copy(
+                        out=raw[:, :, :, :, 3 + f],
+                        in_=chosen[:].rearrange("p s (o g) -> p s o g", o=1).to_broadcast([P, SPREADS, PACK, GROUPS]),
+                    )
                     nc.vector.tensor_tensor(out=rest, in0=rest, in1=piece, op=ALU.subtract)
-            return raw
 
-        def spread_features(raw):
+        def spread_features():
             for s in range(SPREADS):
                 turned = psum.tile([P, PACK, P], BF16, name="turned_f", tag="for_vector", bufs=VB)
                 for t in range(PACK):
@@ -347,7 +370,7 @@ def tile_cfconv_pa_t_kernel(tc, x, distances, W1, b1, W2, b2, out):
 
         def guard_item(c, m):
             if m == 0:
-                h_planes[c] = work.tile([P, PACK, CHUNK], BF16, name="h_planes", tag="planes", bufs=2)
+                h_planes[c] = work.tile([P, PACK, CHUNK], BF16, name="h_planes", tag="planes", bufs=PLANES)
             bank = psum.tile([P, CHUNK], F32, name="bank_v", tag="for_vector", bufs=VB)
             multiply(HIDDEN, c, m, bank)
             if WARM and state["quiet"]:
@@ -475,20 +498,6 @@ def tile_cfconv_pa_t_kernel(tc, x, distances, W1, b1, W2, b2, out):
 
         logged = []
 
-        def plane_ops(c):
-            def product():
-                square_chunk(c)
-
-            def squares_act():
-                square_acts(c)
-
-            def act():
-                exp_chunk(c)
-                grouped = regroup(planes[c])
-                quantise_columns(chunk_cols(c), grouped)
-
-            return [(product, squares_act, 0.5, lambda: True), (None, act, 1.5, None)]
-
         def log_ops(c):
             def act():
                 nc.scalar.activation(out=softs[c][:], in_=softs[c][:], func=ACT.Ln, scale=2.0, bias=tiny[:])
@@ -559,31 +568,34 @@ def tile_cfconv_pa_t_kernel(tc, x, distances, W1, b1, W2, b2, out):
 
         firsts = [sum(BATCHES[:r]) for r in range(len(BATCHES) + 1)]
         HEAD = BATCHES[0]
-        for c in range(min(2, HEAD)):
+        prepare_biases()
+        prepare_window()
+        for c in range(HEAD):
             square_chunk(c)
-            if c == 0:
-                square_acts(0)
+        for c in range(HEAD):
+            square_base(c)
+        for c in range(0, HEAD, 2):
+            for step in (shift_distance, square_next, square_rest):
+                step(c)
+                step(c + 1)
         for c in range(HEAD):
             exp_chunk(c)
+        group_weights(HIDDEN)
+        regrouped = [regroup(planes[0])]
+        quantise_weights(HIDDEN)
+        quantise_columns(chunk_cols(0), regrouped[0])
+        regrouped.append(regroup(planes[1]))
+        for c in range(1, HEAD):
             if c + 1 < HEAD:
-                square_acts(c + 1)
-            if c + 2 < HEAD:
-                square_chunk(c + 2)
-            grouped = regroup(planes[c])
-            if c > 0:
-                quantise_columns(chunk_cols(c - 1), before)
-            before = grouped
-            if c == 1:
-                prepare_layer(HIDDEN)
-        quantise_columns(chunk_cols(HEAD - 1), before)
-        prepare_window()
-        prepare_biases()
-        raw_features = prepare_features()
+                regrouped.append(regroup(planes[c + 1]))
+            quantise_columns(chunk_cols(c), regrouped[c])
+        prepare_features()
         def before_first_squares():
             for quarter in range(GROUPS // PACK):
                 fill_select(quarter)
-            spread_features(raw_features)
-            prepare_layer(FILTER)
+            spread_features()
+            group_weights(FILTER)
+            quantise_weights(FILTER)
 
         hooks = {PACK * HEAD: before_first_squares}
 
@@ -594,12 +606,12 @@ def tile_cfconv_pa_t_kernel(tc, x, distances, W1, b1, W2, b2, out):
             old = list(range(firsts[r - 1], firsts[r])) if r >= 1 else []
             if r >= 1:
                 for c in new:
-                    ops.extend(exp_ops(c) if c >= PLANE_CHUNKS else plane_ops(c))
-            for i in range(max(len(new), len(old))):
+                    ops.extend(exp_ops(c))
+            for i in range(HEADSTART + max(len(new), len(old))):
                 if i < len(old):
                     ops.extend(sigmoid_ops(FILTER, old[i]))
-                if i < len(new):
-                    ops.extend(sigmoid_ops(HIDDEN, new[i]))
+                if 0 <= i - HEADSTART < len(new):
+                    ops.extend(sigmoid_ops(HIDDEN, new[i - HEADSTART]))
             for c in new:
                 ops.extend(log_ops(c))
             for u in finished_units:

@@ -41,6 +41,7 @@ SPREADS = 4
 AHEAD = 4
 MARGIN = 1
 LAG = 1
+RUN = 8
 HEADSTART = 0
 PLANES = 4
 WARM = 0
@@ -242,8 +243,8 @@ def tile_cfconv_pa_t_kernel(tc, x, distances, W1, b1, W2, b2, out):
         def regroup(source):
             grouped = work.tile([P, CHUNK, PACK], BF16, name="grouped", bufs=4, align_bytes=64)
             nc.vector.tensor_copy(
-                out=grouped[:].rearrange("p (c i) t -> p c t i", i=4),
-                in_=source[:].rearrange("p t (c i) -> p c t i", i=4),
+                out=grouped[:].rearrange("p (c i) t -> p c t i", i=RUN),
+                in_=source[:].rearrange("p t (c i) -> p c t i", i=RUN),
             )
             return grouped
 

import math

import concourse.mybir as mybir
from concourse.masks import make_identity

F32 = mybir.dt.float32
BF16 = mybir.dt.bfloat16
I32 = mybir.dt.int32
U32 = mybir.dt.uint32
U8 = mybir.dt.uint8
FP8X4 = mybir.dt.float8_e4m3fn_x4
ACT = mybir.ActivationFunctionType
ALU = mybir.AluOpType

P = 128
PACK = 4
ATOMS = 8
ATOM_ROWS = 144 * ATOMS
PAIRS = ATOM_ROWS * ATOMS
FEATURES = P * PACK
TILES = ATOM_ROWS // P

INV_STEP = 10.0
WIDTH = 0.1
LN2 = math.log(2.0)
TINY = 2.0**-62
CAP = 10.35
FLOOR = 1.0 / (1.0 + math.exp(CAP))
LOG_SCALE = 56

BLOCK = P
CHUNK = 512
BLOCKS = CHUNK // BLOCK
CHUNKS = PAIRS // CHUNK
UNITS = [(0, 2), (2, 2), (4, 2), (6, 2), (8, 1)]
BATCHES = [4, 5, 5, 4]
PLANE_CHUNKS = 4
ROWS = 8
GROUPS = P // ROWS
SPREADS = 4
AHEAD = 4
MARGIN = 1
LAG = 1
RUN = 8
HEADSTART = 0
PLANES = 4
WARM = 0
WARM_TAIL = 0
SOON = 1
CS = 0.5
CE = 0.4
CL = 3.0
SB = 4
VB = 4
SOFTS = 10
SUMS = 2
LATE = [16, 17]

HIDDEN = 0
FILTER = 1

FLOPS = 2 * 2 * PAIRS * FEATURES * FEATURES


def tile_cfconv_pa_t_kernel(tc, x, distances, W1, b1, W2, b2, out):
    nc = tc.nc
    x_rows = x.rearrange("b i f -> (b i) f").rearrange("(q n) f -> q n f", n=TILES)
    out_rows = out.rearrange("b i f -> (b i) f").rearrange("(q n) f -> q n f", n=TILES)
    d_rows = distances.rearrange("b i j -> (b i) j").rearrange("(q n) j -> q n j", n=TILES)

    chunk_unit = []
    chunk_blocks = []
    for u, (first, width) in enumerate(UNITS):
        slots = BLOCKS // width
        for k in range(ATOMS // slots):
            chunk_unit.append((u, k))
            chunk_blocks.append([(first + w, k * slots + s) for s in range(slots) for w in range(width)])

    with tc.manual_schedule(), tc.tile_pool(name="keep", bufs=1) as keep, tc.tile_pool(
        name="work", bufs=2, reuse_waits="tile"
    ) as work, tc.psum_pool(name="psum", bufs=4) as psum:
        d_raw = keep.tile([P, TILES, ATOMS], BF16, name="d_raw")
        nc.sync.dma_start(out=d_raw[:], in_=d_rows)
        raw_weights = []
        raw_biases = []
        for layer, (weight, bias) in enumerate(((W1, b1), (W2, b2))):
            raw_w = work.tile([P, PACK, FEATURES], BF16, name="raw_w", tag="soft", bufs=SOFTS)
            nc.sync.dma_start(out=raw_w[:], in_=weight.rearrange("(p j) f -> p j f", j=PACK))
            raw_weights.append(raw_w)
            raw_b = keep.tile([P, PACK], BF16, name="raw_b%d" % layer)
            nc.sync.dma_start(out=raw_b[:], in_=bias.rearrange("(c m) -> c m", m=PACK))
            raw_biases.append(raw_b)

        centre_int = keep.tile([P, PACK], I32, name="centre_int")
        nc.gpsimd.iota(centre_int[:], pattern=[[1, PACK]], base=0, channel_multiplier=PACK)
        window = keep.tile([P, 2 * P - ROWS], BF16, name="window")
        nc.gpsimd.memset(window[:], 0.0)
        identity_b = keep.tile([P, P], BF16, name="identity_b")
        make_identity(nc, identity_b[:])
        whole = keep.tile([P, PACK], F32, name="whole")
        for t in range(PACK):
            nc.gpsimd.memset(whole[:, t : t + 1], float(t * (t - 1)))
        tiny = keep.tile([P, 1], F32, name="tiny")
        nc.gpsimd.memset(tiny[:], TINY)
        raw = keep.tile([P, SPREADS, PACK, GROUPS, ROWS], BF16, name="raw_features")
        nc.gpsimd.memset(raw[:], 1.0)
        minus_t = keep.tile([P, PACK, 1], F32, name="minus_t")
        for t in range(PACK):
            nc.gpsimd.memset(raw[:, :, t, :, 5], float(t))
            nc.gpsimd.memset(minus_t[:, t, :], -float(t))
        chosen = keep.tile([P, SPREADS, GROUPS], BF16, name="chosen")
        nc.gpsimd.memset(chosen[:, 3, ATOMS:GROUPS], 0.0)
        identity = keep.tile([P, P], F32, name="identity")
        make_identity(nc, identity[:])
        centre = keep.tile([P, PACK], F32, name="centre")
        nc.vector.tensor_copy(out=centre[:], in_=centre_int[:])
        minus_centre = keep.tile([P, PACK], F32, name="minus_centre")
        nc.vector.tensor_scalar(out=minus_centre[:], in0=centre[:], scalar1=-1.0, scalar2=None, op0=ALU.mult)

        moving_codes = keep.tile([P, PAIRS], U32, name="moving_codes", align_bytes=64)
        moving_scales = keep.tile([P, PAIRS], U8, name="moving_scales", align_bytes=64)
        weight_codes = [
            keep.tile([P, FEATURES], U32, name="w1_codes", align_bytes=64),
            keep.tile([P, FEATURES], U32, name="w2_codes", align_bytes=64),
        ]
        weight_scales = [
            keep.tile([P, FEATURES], U8, name="w1_scales", align_bytes=64),
            keep.tile([P, FEATURES], U8, name="w2_scales", align_bytes=64),
        ]
        exp_bias = keep.tile([P, PACK], F32, name="exp_bias")
        minus_bias = [keep.tile([P, PACK], F32, name="minus_b1"), keep.tile([P, PACK], F32, name="minus_b2")]
        guard_bias = keep.tile([P, PACK], F32, name="guard_bias")
        guard_bias2 = keep.tile([P, PACK], F32, name="guard_bias2")
        limit = keep.tile([P, PACK], F32, name="limit")
        capped = [[c for c in range(CHUNKS) if chunk_unit[c][0] == u and c not in LATE] for u in range(len(UNITS))]
        guarded = [[c for c in range(CHUNKS) if chunk_unit[c][0] == u and c in LATE] for u in range(len(UNITS))]
        offset = {}
        for steps in sorted(set(len(chunks) for chunks in capped if chunks)):
            offset[steps] = keep.tile([P, PACK], F32, name="offset%d" % steps)

        def quantise_columns(cols, grouped):
            nc.vector.quantize_mx(
                out=moving_codes[:, cols].bitcast(FP8X4),
                scales=moving_scales[:, cols],
                in_=grouped[:].rearrange("p w t -> p (w t)"),
            )

        def chunk_cols(c):
            return slice(c * CHUNK, (c + 1) * CHUNK)

        grouped_weights = {}

        def group_weights(layer):
            sign = -1.0 if layer == HIDDEN else 1.0
            grouped_w = work.tile([P, PACK, P, PACK], BF16, name="grouped_w", tag="grouped", bufs=4, align_bytes=64)
            for m in range(PACK):
                nc.vector.tensor_scalar(
                    out=grouped_w[:, m, :, :],
                    in0=raw_weights[layer][:].rearrange("p j (c m) -> p m c j", m=PACK)[:, m, :, :],
                    scalar1=sign, scalar2=None, op0=ALU.mult,
                )
            grouped_weights[layer] = grouped_w

        def quantise_weights(layer):
            nc.vector.quantize_mx(
                out=weight_codes[layer][:].bitcast(FP8X4),
                scales=weight_scales[layer][:],
                in_=grouped_weights[layer][:].rearrange("p m c j -> p (m c j)"),
            )

        def prepare_biases():
            nc.gpsimd.tensor_scalar(out=exp_bias[:], in0=whole[:], scalar1=-WIDTH, scalar2=0.0, op0=ALU.mult, op1=ALU.add)
            for layer in (HIDDEN, FILTER):
                nc.gpsimd.tensor_scalar(
                    out=minus_bias[layer][:], in0=raw_biases[layer][:], scalar1=-1.0, scalar2=0.0, op0=ALU.mult, op1=ALU.add
                )
            nc.gpsimd.tensor_scalar(
                out=guard_bias[:], in0=raw_biases[HIDDEN][:], scalar1=-1.0, scalar2=LN2, op0=ALU.mult, op1=ALU.add
            )
            nc.gpsimd.tensor_scalar(
                out=guard_bias2[:], in0=raw_biases[FILTER][:], scalar1=-1.0, scalar2=LN2, op0=ALU.mult, op1=ALU.add
            )
            nc.gpsimd.tensor_scalar(
                out=limit[:], in0=raw_biases[FILTER][:], scalar1=1.0, scalar2=-CAP, op0=ALU.mult, op1=ALU.add
            )
            for steps in sorted(offset):
                nc.gpsimd.tensor_scalar(
                    out=offset[steps][:], in0=raw_biases[FILTER][:], scalar1=-float(steps),
                    scalar2=steps * (CAP + LN2) - steps * LOG_SCALE * LN2 / ATOMS, op0=ALU.mult, op1=ALU.add,
                )

        squares = {}
        spreads = {}
        planes = {}

        def square_chunk(c):
            spread = psum.tile([P, CHUNK], BF16, name="spread", tag="for_scalar", bufs=SB)
            for i, (n, j) in enumerate(chunk_blocks[c]):
                nc.tensor.transpose(
                    spread[:, i * BLOCK : (i + 1) * BLOCK],
                    d_raw[:, n, j : j + 1].to_broadcast([P, P]),
                    identity_b[:],
                )
            spreads[c] = spread

        shifted = {}

        def square_base(c):
            squares[c] = work.tile([P, PACK, CHUNK], F32, name="sq", tag="soft", bufs=SOFTS)
            nc.scalar.activation(
                out=squares[c][:, 0, :], in_=spreads[c][:], func=ACT.Square, scale=INV_STEP, bias=minus_centre[:, 0:1]
            )

        def shift_distance(c):
            shifted[c] = work.tile([P, CHUNK], F32, name="shifted")
            nc.vector.tensor_scalar(
                out=shifted[c][:], in0=spreads[c][:], scalar1=INV_STEP, scalar2=minus_centre[:, 1:2],
                op0=ALU.mult, op1=ALU.add,
            )

        def square_next(c):
            nc.vector.tensor_tensor(out=squares[c][:, 1, :], in0=shifted[c][:], in1=shifted[c][:], op=ALU.mult)

        def square_rest(c):
            sq = squares[c]
            for t in range(2, PACK):
                nc.vector.scalar_tensor_tensor(
                    out=sq[:, t, :], in0=sq[:, 1, :], scalar=t / (t - 1.0), in1=sq[:, 0, :],
                    op0=ALU.mult, op1=ALU.subtract,
                )

        def exp_chunk(c):
            sq = squares[c]
            e_planes = work.tile([P, PACK, CHUNK], BF16, name="e_planes", tag="planes", bufs=PLANES)
            nc.scalar.activation(out=e_planes[:, 0:2, :], in_=sq[:, 0:2, :], func=ACT.Exp, scale=-WIDTH)
            for t in range(2, PACK):
                nc.scalar.activation(
                    out=e_planes[:, t, :], in_=sq[:, t, :], func=ACT.Exp,
                    scale=-WIDTH * (t - 1), bias=exp_bias[:, t : t + 1],
                )
            planes[c] = e_planes

        def regroup(source):
            grouped = work.tile([P, CHUNK, PACK], BF16, name="grouped", bufs=4, align_bytes=64)
            nc.vector.tensor_copy(
                out=grouped[:].rearrange("p (c i) t -> p c t i", i=RUN),
                in_=source[:].rearrange("p t (c i) -> p c t i", i=RUN),
            )
            return grouped

        select = keep.tile([P, GROUPS, P], BF16, name="select")
        features = keep.tile([P, SPREADS, CHUNK], BF16, name="features")

        MID = P - ROWS

        def prepare_window():
            w32 = keep.tile([P, 2], F32, name="w32")
            nc.vector.memset(window[:, MID : MID + 3], 1.0)
            nc.vector.tensor_scalar(out=w32[:, 0:1], in0=centre[:, 0:1], scalar1=-20.0, scalar2=None, op0=ALU.mult)
            nc.vector.tensor_tensor(out=w32[:, 1:2], in0=centre[:, 0:1], in1=centre[:, 0:1], op=ALU.mult)
            nc.vector.tensor_scalar(out=window[:, MID + 5 : MID + 6], in0=centre[:, 0:1], scalar1=2.0, scalar2=None, op0=ALU.mult)
            nc.vector.tensor_copy(out=window[:, MID + 3 : MID + 7 : 3], in_=w32[:])
            nc.vector.tensor_tensor(
                out=window[:, MID + 4 : MID + 8 : 3], in0=w32[:], in1=window[:, MID + 3 : MID + 7 : 3], op=ALU.subtract
            )

        def fill_select(quarter):
            turned = psum.tile([P, PACK, P], BF16, name="turned_w", tag="for_vector", bufs=VB)
            for i in range(PACK):
                g = quarter * PACK + i
                nc.tensor.transpose(turned[:, i, :], window[:, MID - ROWS * g : MID - ROWS * g + P], identity_b[:])
            nc.vector.tensor_copy(out=select[:, quarter * PACK : (quarter + 1) * PACK, :], in_=turned[:])

        def prepare_features():
            for s in range(3):
                nc.vector.tensor_copy(
                    out=chosen[:, s, :].rearrange("p (j n) -> p j n", n=2),
                    in_=d_raw[:, 2 * s + 2 : 2 * s + 4, :].rearrange("p n j -> p j n"),
                )
            nc.vector.tensor_copy(out=chosen[:, 3, 0:ATOMS], in_=d_raw[:, 8, :])
            shape = [P, PACK, SPREADS * GROUPS]
            z = keep.tile(shape, F32, name="z")
            nc.vector.scalar_tensor_tensor(
                out=z[:], in0=chosen[:].rearrange("p s (o g) -> p o (s g)", o=1).to_broadcast(shape), scalar=INV_STEP,
                in1=minus_t[:].to_broadcast(shape), op0=ALU.mult, op1=ALU.add,
            )
            z2 = keep.tile(shape, F32, name="z2")
            nc.vector.tensor_tensor(out=z2[:], in0=z[:], in1=z[:], op=ALU.mult)
            rest = z2[:].rearrange("p t (s g) -> p s t g", g=GROUPS)
            for f in range(3):
                piece = raw[:, :, :, :, f]
                nc.vector.tensor_copy(out=piece, in_=rest)
                if f < 2:
                    nc.vector.tensor_copy(
                        out=raw[:, :, :, :, 3 + f],
                        in_=chosen[:].rearrange("p s (o g) -> p s o g", o=1).to_broadcast([P, SPREADS, PACK, GROUPS]),
                    )
                    nc.vector.tensor_tensor(out=rest, in0=rest, in1=piece, op=ALU.subtract)

        def spread_features():
            for s in range(SPREADS):
                turned = psum.tile([P, PACK, P], BF16, name="turned_f", tag="for_vector", bufs=VB)
                for t in range(PACK):
                    nc.tensor.transpose(turned[:, t, :], raw[:, s, t, :, :].rearrange("p g r -> p (g r)"), identity_b[:])
                nc.vector.tensor_copy(
                    out=features[:, s, :].rearrange("p (c t) -> p c t", t=PACK), in_=turned[:].rearrange("p t c -> p c t")
                )

        def multiply(layer, c, m, bank):
            feats = slice(m * P, (m + 1) * P)
            cols = chunk_cols(c)
            nc.tensor.matmul_mx(
                out=bank[:],
                lhsT=weight_codes[layer][:, feats].bitcast(FP8X4),
                lhsT_scale=weight_scales[layer][:, feats],
                rhs=moving_codes[:, cols].bitcast(FP8X4),
                rhs_scale=moving_scales[:, cols],
                start=True,
                stop=True,
            )

        items = []
        state = {"next": 0, "credit": 0.0}
        waiting = []
        turns = []
        state["turn"] = 0
        state["quiet"] = False

        def run_turn():
            if state["turn"] < len(turns):
                turns[state["turn"]]()
                state["turn"] += 1
                return True
            return False

        def run_waiting():
            for entry in list(waiting):
                entry[0] -= 1
                if entry[0] == 0:
                    waiting.remove(entry)
                    entry[1]()

        def run_item():
            if state["next"] >= len(items):
                return False
            state["next"] += 1
            items[state["next"] - 1][2]()
            run_waiting()
            run_turn()
            return True

        def run_items(credit):
            state["credit"] += credit
            while state["credit"] >= 1.0:
                state["credit"] -= 1.0
                if not run_item():
                    run_waiting()
                    run_turn()

        def finish_items(kind, c):
            while any(k == kind and d == c for k, d, f in items[state["next"] :]):
                run_item()

        def finish(kind, c):
            finish_items(kind, c)
            while waiting:
                run_waiting()

        softs = {}
        h_planes = {}

        def guard_item(c, m):
            if m == 0:
                h_planes[c] = work.tile([P, PACK, CHUNK], BF16, name="h_planes", tag="planes", bufs=PLANES)
            bank = psum.tile([P, CHUNK], F32, name="bank_v", tag="for_vector", bufs=VB)
            multiply(HIDDEN, c, m, bank)
            if WARM and state["quiet"]:
                multiply(HIDDEN, c, m, bank)
            nc.vector.scalar_tensor_tensor(
                out=h_planes[c][:, m, :], in0=bank[:], scalar=guard_bias[:, m : m + 1], in1=softs[c][:, m, :],
                op0=ALU.add, op1=ALU.min,
            )
            if m == PACK - 1:
                def gather():
                    grouped = regroup(h_planes[c])
                    waiting.append([LAG, lambda: quantise_columns(chunk_cols(c), grouped)])

                waiting.append([LAG + 1, gather])

        sums = {}
        products = {}

        def merge(u, columns):
            half = columns // 2
            nc.vector.tensor_tensor(
                out=products[u][:, :, 0:half], in0=products[u][:, :, 0:half], in1=products[u][:, :, half:columns], op=ALU.mult
            )
            if half > UNITS[u][1] * P:
                waiting.append([1, lambda: merge(u, half)])

        def filter_item(c, m):
            u, k = chunk_unit[c]
            if c == capped[u][0] and m == 0:
                sums[u] = work.tile([P, PACK, CHUNK], F32, name="sums", bufs=SUMS)
                products[u] = work.tile([P, PACK, CHUNK], F32, name="products", bufs=SUMS)
            bank = psum.tile([P, CHUNK], F32, name="bank_v", tag="for_vector", bufs=VB)
            multiply(FILTER, c, m, bank)
            if c == capped[u][0]:
                nc.vector.tensor_scalar(
                    out=sums[u][:, m, :], in0=bank[:], scalar1=limit[:, m : m + 1],
                    scalar2=offset[len(capped[u])][:, m : m + 1], op0=ALU.min, op1=ALU.add,
                )
            else:
                nc.vector.scalar_tensor_tensor(
                    out=sums[u][:, m, :], in0=bank[:], scalar=limit[:, m : m + 1], in1=sums[u][:, m, :],
                    op0=ALU.min, op1=ALU.add,
                )
            if m == PACK - 1:
                if c == capped[u][0]:
                    nc.vector.tensor_scalar(
                        out=products[u][:], in0=softs[c][:], scalar1=FLOOR,
                        scalar2=2.0 ** (LOG_SCALE * len(capped[u]) // ATOMS), op0=ALU.max, op1=ALU.mult,
                    )
                else:
                    nc.vector.scalar_tensor_tensor(
                        out=products[u][:], in0=softs[c][:], scalar=FLOOR, in1=products[u][:], op0=ALU.max, op1=ALU.mult
                    )
                if c == capped[u][-1]:
                    waiting.append([1, lambda: merge(u, CHUNK)])

        def late_item(c, m):
            bank = psum.tile([P, CHUNK], F32, name="bank_v", tag="for_vector", bufs=VB)
            multiply(FILTER, c, m, bank)
            if WARM_TAIL:
                multiply(FILTER, c, m, bank)
            nc.vector.scalar_tensor_tensor(
                out=softs[c][:, m, :], in0=bank[:], scalar=guard_bias2[:, m : m + 1], in1=softs[c][:, m, :],
                op0=ALU.add, op1=ALU.min,
            )

        def push_output(u, w):
            first, width = UNITS[u]
            n = first + w
            slots = BLOCKS // width
            held = {}
            x_tile = work.tile([P, FEATURES], BF16, name="x_tile", bufs=4)
            nc.sync.dma_start(out=x_tile[:], in_=x_rows[:, n, :])

            def turn(m):
                if m == 0:
                    held["bank"] = psum.tile([P, PACK, P], F32, name="turned", tag="for_vector", bufs=VB)
                tiles = [sums[u]] if capped[u] else []
                tiles.extend([softs[c] for c in guarded[u]])
                terms = [tile[:, m, (s * width + w) * P : (s * width + w + 1) * P] for tile in tiles for s in range(slots)]
                if capped[u]:
                    terms.append(products[u][:, m, w * P : (w + 1) * P])
                for i, term in enumerate(terms):
                    nc.tensor.matmul(
                        held["bank"][:, m, :], term, identity[:],
                        start=(i == 0), stop=(i == len(terms) - 1), is_transpose=True,
                    )
                if m == PACK - 1:
                    result = work.tile([P, FEATURES], F32, name="result")
                    nc.vector.scalar_tensor_tensor(
                        out=result[:].rearrange("p (c m) -> p c m", m=PACK),
                        in0=held["bank"][:].rearrange("p m c -> p c m"),
                        scalar=-1.0,
                        in1=x_tile[:].rearrange("p (c m) -> p c m", m=PACK),
                        op0=ALU.mult,
                        op1=ALU.mult,
                    )
                    nc.sync.dma_start(out=out_rows[:, n, :], in_=result[:])

            return [lambda m=m: turn(m) for m in range(PACK)]

        def sigmoid_ops(layer, c):
            held = {}

            def product(m):
                if layer == FILTER and m == 0:
                    for d in range(c, min(c + MARGIN + 1, CHUNKS)):
                        finish_items("hidden", d)
                    finish("hidden", c)
                bank = psum.tile([P, CHUNK], F32, name="bank_s", tag="for_scalar", bufs=SB)
                multiply(layer, c, m, bank)
                held[m] = bank

            def act(m):
                if m == 0:
                    softs[c] = work.tile([P, PACK, CHUNK], F32, name="soft", bufs=SOFTS)
                nc.scalar.activation(
                    out=softs[c][:, m, :], in_=held[m][:], func=ACT.Sigmoid, bias=minus_bias[layer][:, m : m + 1]
                )
                if layer == FILTER and m == PACK - 1 and c not in LATE:
                    for q in range(PACK):
                        items.append(("filter", c, lambda q=q: filter_item(c, q)))

            return [(lambda m=m: product(m), lambda m=m: act(m), CS, lambda: layer == HIDDEN or min(c + MARGIN, CHUNKS - 1) in logged or (c in logged and c + 1 in firsts)) for m in range(PACK)]

        logged = []

        def log_ops(c):
            def act():
                nc.scalar.activation(out=softs[c][:], in_=softs[c][:], func=ACT.Ln, scale=2.0, bias=tiny[:])
                logged.append(c)
                for m in range(PACK):
                    items.append(("hidden", c, lambda m=m: guard_item(c, m)))

            return [(None, act, CL, None)]


        def exp_ops(c):
            held = {}

            def product(i):
                number = (c - PLANE_CHUNKS) * BLOCKS + i
                bank = psum.tile([P, CHUNK], F32, name="bank_x", tag="for_scalar", bufs=SB)
                nc.tensor.matmul(
                    bank[:], select[:, number % GROUPS, :], features[:, number // GROUPS, :], start=True, stop=True
                )
                held[i] = bank

            def act(i):
                if i == 0:
                    held["grouped"] = work.tile([P, CHUNK, PACK], BF16, name="grouped", bufs=4, align_bytes=64)
                nc.scalar.activation(
                    out=held["grouped"][:, i * BLOCK : (i + 1) * BLOCK, :].rearrange("p c t -> p (c t)"),
                    in_=held[i][:], func=ACT.Exp, scale=-WIDTH,
                )
                if i == BLOCKS - 1:
                    quantise_columns(chunk_cols(c), held["grouped"])

            return [(lambda i=i: product(i), lambda i=i: act(i), CE, lambda: True) for i in range(BLOCKS)]

        later = []

        def late_log_ops(c):
            u, k = chunk_unit[c]
            last = c == guarded[u][-1]
            held = {}

            def guard_and_turn(m):
                late_item(c, m)
                if last and m == PACK - 1:
                    for w in range(UNITS[u][1]):
                        turns.extend(push_output(u, w))

            def act(m):
                nc.scalar.activation(
                    out=softs[c][:, m, :], in_=softs[c][:, m, :], func=ACT.Ln, scale=2.0, bias=tiny[:]
                )
                items.append(("late", c, lambda: guard_and_turn(m)))

            return [(None, lambda m=m: act(m), 0.5, None) for m in range(PACK)]

        def product_log_ops(u):
            def act():
                for c in capped[u]:
                    finish("filter", c)
                while waiting:
                    run_waiting()
                merged = products[u][:, :, 0 : UNITS[u][1] * P]
                nc.scalar.activation(out=merged, in_=merged, func=ACT.Ln)
                if not guarded[u]:
                    for w in range(UNITS[u][1]):
                        later.append(lambda w=w: turns.extend(push_output(u, w)))

            return [(None, act, 2.0, None)]

        firsts = [sum(BATCHES[:r]) for r in range(len(BATCHES) + 1)]
        HEAD = BATCHES[0]
        prepare_biases()
        prepare_window()
        for c in range(HEAD):
            square_chunk(c)
        for c in range(HEAD):
            square_base(c)
        for c in range(0, HEAD, 2):
            for step in (shift_distance, square_next, square_rest):
                step(c)
                step(c + 1)
        for c in range(HEAD):
            exp_chunk(c)
        group_weights(HIDDEN)
        regrouped = [regroup(planes[0])]
        quantise_weights(HIDDEN)
        quantise_columns(chunk_cols(0), regrouped[0])
        regrouped.append(regroup(planes[1]))
        for c in range(1, HEAD):
            if c + 1 < HEAD:
                regrouped.append(regroup(planes[c + 1]))
            quantise_columns(chunk_cols(c), regrouped[c])
        prepare_features()
        def before_first_squares():
            for quarter in range(GROUPS // PACK):
                fill_select(quarter)
            spread_features()
            group_weights(FILTER)
            quantise_weights(FILTER)

        hooks = {PACK * HEAD: before_first_squares}

        ops = []
        finished_units = []
        for r in range(len(BATCHES) + 1):
            new = list(range(firsts[r], firsts[r + 1])) if r < len(BATCHES) else []
            old = list(range(firsts[r - 1], firsts[r])) if r >= 1 else []
            if r >= 1:
                for c in new:
                    ops.extend(exp_ops(c))
            for i in range(HEADSTART + max(len(new), len(old))):
                if i < len(old):
                    ops.extend(sigmoid_ops(FILTER, old[i]))
                if 0 <= i - HEADSTART < len(new):
                    ops.extend(sigmoid_ops(HIDDEN, new[i - HEADSTART]))
            for c in new:
                ops.extend(log_ops(c))
            for u in finished_units:
                ops.extend(product_log_ops(u))
            for c in old:
                if c in LATE:
                    ops.extend(late_log_ops(c))
            finished_units = [chunk_unit[c][0] for c in old if c in [chunks[-1] for chunks in capped if chunks]]
            if not new or SOON:
                for u in finished_units:
                    ops.extend(product_log_ops(u))
                finished_units = []

        banked = [op for op in ops if op[0] is not None]
        ahead = 0
        used = 0
        for op in ops:
            ready = list(later)
            later.clear()
            while ahead < len(banked) and ahead < used + AHEAD and banked[ahead][3]():
                if ahead in hooks:
                    hooks[ahead]()
                banked[ahead][0]()
                ahead += 1
            op[1]()
            state["quiet"] = op[0] is None
            if op[0] is not None:
                used += 1
            run_items(op[2])
            for f in ready:
                f()
        for f in later:
            f()
        while run_item() or run_turn():
            pass
